import numpy as np
import ml_dtypes


def mxq(x, axis, fmt="e4m3"):
    dtype, down = {"e4m3": (ml_dtypes.float8_e4m3fn, 7), "e5m2": (ml_dtypes.float8_e5m2, 14)}[fmt]
    v = np.moveaxis(np.asarray(x, np.float32).astype(ml_dtypes.bfloat16).astype(np.float64), axis, -1)
    blocks = v.reshape(v.shape[:-1] + (-1, 32))
    amax = np.abs(blocks).max(-1, keepdims=True)
    byte = np.maximum(np.where(amax > 0, np.frexp(amax)[1] - 1 + 127, 0) - down, 1)
    scale = np.exp2(byte - 127.0)
    codes = (blocks / scale).astype(np.float32).astype(dtype).astype(np.float64)
    return np.moveaxis((codes * scale).reshape(v.shape), -1, axis)


WIDE = False


def mx_kscale(k):
    if not WIDE:
        return np.ones(k)
    levels = np.array([10, -10, 5, -5, 0])
    a = np.random.permutation(np.resize(levels, k // 512 * 4)).reshape(k // 512, 4)
    idx = np.arange(k)
    return np.exp2(a[idx // 512, idx % 128 // 32])


BF16 = ml_dtypes.bfloat16


def bf(x):
    return np.asarray(x, np.float32).astype(BF16)


def f64(x):
    return np.asarray(x).astype(np.float64)


E2M1 = np.array([0.0, 0.5, 1.0, 1.5, 2.0, 3.0, 4.0, 6.0, -0.0, -0.5, -1.0, -1.5, -2.0, -3.0, -4.0, -6.0])


def pack_weight(w, fmt):
    k, n = w.shape
    w = f64(bf(w)).reshape(k // 32, 32, n)
    amax = np.abs(w).max(1)
    if fmt == "e4m3":
        byte = np.frexp(amax)[1] - 1 + 127 - 7
    else:
        mant, ex = np.frexp(amax / 6.0)
        byte = np.where(mant > 0.5, ex, ex - 1) + 127
    byte = np.clip(np.where(amax > 0, byte, 1), 1, 254)
    scaled = (w * np.exp2(127.0 - byte)[:, None, :]).reshape(k, n).astype(np.float32)
    by_word = np.ascontiguousarray(scaled.reshape(k // 512, 128, 4, n).transpose(0, 1, 3, 2))
    if fmt == "e4m3":
        words = by_word.astype(ml_dtypes.float8_e4m3fn).view(np.uint8)
    else:
        c = by_word.astype(ml_dtypes.float4_e2m1fn).view(np.uint8) & 0xF
        words = c[..., 0::2] | (c[..., 1::2] << 4)
    return np.ascontiguousarray(words), np.ascontiguousarray(byte.astype(np.uint8).reshape(k // 512, 16, n))


def unpack_weight(words, scales, fmt):
    g, p, n, _ = words.shape
    if fmt == "e4m3":
        vals = np.ascontiguousarray(words).view(ml_dtypes.float8_e4m3fn).astype(np.float64)
    else:
        nib = np.empty((g, p, n, 4), np.uint8)
        nib[..., 0::2] = words & 0xF
        nib[..., 1::2] = words >> 4
        vals = E2M1[nib]
    vals = vals * np.repeat(np.exp2(scales.astype(np.float64) - 127.0), 8, axis=1)[..., None]
    return vals.transpose(0, 1, 3, 2).reshape(g * 512, n)


B, D_IN, D_H, C = 8192, 512, 512, 128
TAU, T1, T2 = 0.5, 3, 3
G, GB = 3.0, 3.0
FMT = "e4m3"


def inv_apprx(v, t, m):
    a = 2.0 - (2.0 / m) * v
    b = 1.0 - (2.0 / m) * v
    for _ in range(t):
        b = b * b
        a = a * (1.0 + b)
    return (2.0 / m) * a


def comp_max_tau(p, tau, t1, t2):
    res = np.concatenate([p, np.full((p.shape[0], 1), tau)], axis=1)
    for i in range(t1):
        res = res * res
        sum_res = res.sum(axis=1)
        m = (2.0 + tau * tau) if i == 0 else 2.0
        res = res * inv_apprx(sum_res, t2, m)[:, None]
    return res[:, -1]


def softmax(z):
    e = np.exp(z - z.max(-1, keepdims=True))
    return e / e.sum(-1, keepdims=True)


def mlp(xq, W1_words, W1_scales, b1, W2_words, W2_scales, b2):
    h = np.maximum((xq @ unpack_weight(W1_words, W1_scales, FMT)) + f64(b1), 0.0)
    return softmax((mxq(h, 1, "e4m3") @ unpack_weight(W2_words, W2_scales, FMT)) + f64(b2))


def setup_inputs():
    s, t = mx_kscale(D_IN), mx_kscale(D_H)
    x = bf(np.random.standard_normal((B, D_IN)) * s)
    W1o_words, W1o_scales = pack_weight(np.random.standard_normal((D_IN, D_H)) / np.sqrt(D_IN) / s[:, None] * t, FMT)
    b1o = bf(np.random.standard_normal(D_H) * 0.2 * t)
    W2o_words, W2o_scales = pack_weight(np.random.standard_normal((D_H, C)) * G / np.sqrt(D_H) / t[:, None], FMT)
    b2o = bf(np.random.standard_normal(C) * GB)
    W1f_words, W1f_scales = pack_weight(np.random.standard_normal((D_IN, D_H)) / np.sqrt(D_IN) / s[:, None] * t, FMT)
    b1f = bf(np.random.standard_normal(D_H) * 0.2 * t)
    W2f_words, W2f_scales = pack_weight(np.random.standard_normal((D_H, C)) * G / np.sqrt(D_H) / t[:, None], FMT)
    b2f = bf(np.random.standard_normal(C) * GB)
    return {"x": x,
            "W1o_words": W1o_words, "W1o_scales": W1o_scales,
            "b1o": b1o,
            "W2o_words": W2o_words, "W2o_scales": W2o_scales,
            "b2o": b2o,
            "W1f_words": W1f_words, "W1f_scales": W1f_scales,
            "b1f": b1f,
            "W2f_words": W2f_words, "W2f_scales": W2f_scales,
            "b2f": b2f}


def reference(x, W1o_words, W1o_scales, b1o, W2o_words, W2o_scales, b2o, W1f_words, W1f_scales, b1f, W2f_words, W2f_scales, b2f):
    xq = mxq(f64(x), 1, "e4m3")
    x1 = mlp(xq, W1o_words, W1o_scales, b1o, W2o_words, W2o_scales, b2o)
    x2 = mlp(xq, W1f_words, W1f_scales, b1f, W2f_words, W2f_scales, b2f)
    cond_in = comp_max_tau(x1, TAU, T1, T2)
    return x1 * (1.0 - cond_in[:, None]) + x2 * cond_in[:, None]

@@ -1,0 +1,394 @@
+from contextlib import ExitStack
+
+import concourse.mybir as mybir
+from concourse.masks import make_identity
+
+F32 = mybir.dt.float32
+BF16 = mybir.dt.bfloat16
+I32 = mybir.dt.int32
+U32 = mybir.dt.uint32
+U8 = mybir.dt.uint8
+FP8X4 = mybir.dt.float8_e4m3fn_x4
+ALU = mybir.AluOpType
+ACT = mybir.ActivationFunctionType
+AXIS = mybir.AxisListType
+
+P = 128
+PACK = 4
+TOKENS, D_IN, D_H, CLASSES = 8192, 512, 512, 128
+N_TILES = TOKENS // P
+PAIR = 2
+N_UNITS = N_TILES // PAIR
+NET_O, NET_F = 0, 1
+LEAD = 8
+N_JOBS = N_UNITS + LEAD
+BLOCK_TILES = LEAD * PAIR
+UNITS_PER_LOAD = 2
+LOAD_AHEAD = 4
+
+AT_LAYER1 = 2
+AT_TRANSPOSE_H = 3
+AT_LAYER2 = 5
+AT_SOFTMAX = 6
+AT_GATE = 7
+AT_PREPARE = 12
+AT_BLEND = 13
+
+TAU = 0.5
+C0 = 2.0 / (2.0 + TAU * TAU)
+
+FLOPS = 2 * 2 * TOKENS * (D_IN * D_H + D_H * CLASSES)
+
+
+def members(job):
+    found = []
+    if 0 <= job < N_UNITS:
+        found.append((NET_O, job))
+    if 0 <= job - LEAD < N_UNITS:
+        found.append((NET_F, job - LEAD))
+    return found
+
+
+def tile_combnethe_pa_t_kernel(
+    tc, x, W1o_words, W1o_scales, b1o, W2o_words, W2o_scales, b2o,
+    W1f_words, W1f_scales, b1f, W2f_words, W2f_scales, b2f, out,
+):
+    nc = tc.nc
+    weights_in = {
+        NET_O: (W1o_words, W1o_scales, b1o, W2o_words, W2o_scales, b2o),
+        NET_F: (W1f_words, W1f_scales, b1f, W2f_words, W2f_scales, b2f),
+    }
+    x_by_tile = x.rearrange("(p i) k -> p i k", i=N_TILES)
+    out_by_tile = out.rearrange("(p i) c -> p i c", i=N_TILES)
+
+    with ExitStack() as ctx:
+        ctx.enter_context(tc.manual_schedule())
+        keep = ctx.enter_context(tc.tile_pool(name="keep", bufs=1))
+        loads = ctx.enter_context(tc.tile_pool(name="loads", bufs=4))
+        x_grouped_pool = ctx.enter_context(tc.tile_pool(name="x_grouped", bufs=4))
+        pre_pool = ctx.enter_context(tc.tile_pool(name="pre", bufs=6))
+        h_grouped_pool = ctx.enter_context(tc.tile_pool(name="h_grouped", bufs=8))
+        h_packed_pool = ctx.enter_context(tc.tile_pool(name="h_packed", bufs=4))
+        logit_pool = ctx.enter_context(tc.tile_pool(name="logit", bufs=3))
+        exp_f_pool = ctx.enter_context(tc.tile_pool(name="exp_f", bufs=9))
+        power_pool = ctx.enter_context(tc.tile_pool(name="power", bufs=2))
+        blend_pool = ctx.enter_context(tc.tile_pool(name="blend", bufs=4))
+        gate_pool = ctx.enter_context(tc.tile_pool(name="gate", bufs=2))
+        psum_x = ctx.enter_context(tc.psum_pool(name="psum_x", bufs=1))
+        psum_z = ctx.enter_context(tc.psum_pool(name="psum_z", bufs=4))
+        psum_h = ctx.enter_context(tc.psum_pool(name="psum_h", bufs=2))
+        psum_l = ctx.enter_context(tc.psum_pool(name="psum_l", bufs=1))
+
+        identity = keep.tile([P, P], F32, name="identity")
+        make_identity(nc, identity[:])
+
+        x_words = keep.tile([P, TOKENS], U32, name="x_words", align_bytes=64)
+        x_scales = keep.tile([P, TOKENS], U8, name="x_scales", align_bytes=64)
+        exp_o = keep.tile([P, N_TILES, CLASSES], F32, name="exp_o")
+        sum_o = keep.tile([P, N_TILES], F32, name="sum_o")
+        sum_o2 = keep.tile([P, N_TILES], F32, name="sum_o2")
+        sum_o4 = keep.tile([P, N_TILES], F32, name="sum_o4")
+        sum_o8 = keep.tile([P, N_TILES], F32, name="sum_o8")
+        sum_f = keep.tile([P, N_TILES], F32, name="sum_f")
+        inv_sum_o = keep.tile([P, N_TILES], F32, name="inv_sum_o")
+        cond = keep.tile([P, N_TILES], F32, name="cond")
+        coef_o = keep.tile([P, N_TILES], F32, name="coef_o")
+
+        w1_words, w1_scales, w2_words, w2_scales = {}, {}, {}, {}
+        b1_raw, b1_sorted = {}, {}
+        b2_raw = keep.tile([P, 2, CLASSES], BF16, name="b2_raw")
+        b2_both = keep.tile([P, 2, CLASSES], F32, name="b2_both")
+
+        def load_weight(words_in, scales_in, width, name):
+            words = keep.tile([P, width], U32, name=name + "_words", align_bytes=64)
+            nc.sync.dma_start(
+                out=words[:].bitcast(I32), in_=words_in[0].rearrange("p n t -> p (n t)").bitcast(I32)
+            )
+            scales = keep.tile([P, width], U8, name=name + "_scales", align_bytes=64)
+            nc.vector.memset(scales[:].bitcast(I32), 0)
+            for r in range(4):
+                nc.sync.dma_start(
+                    out=scales[:].bitcast(I32)[r:P:32, :], in_=scales_in[0].bitcast(I32)[r:16:4, :]
+                )
+            return words, scales
+
+        def load_network(net):
+            w1w, w1s, b1, w2w, w2s, b2 = weights_in[net]
+            w1_words[net], w1_scales[net] = load_weight(w1w, w1s, D_H, "w1_%d" % net)
+            b1_raw[net] = keep.tile([P, D_H], BF16, name="b1_raw_%d" % net)
+            nc.sync.dma_start(out=b1_raw[net][:], in_=b1.partition_broadcast(P))
+            w2_words[net], w2_scales[net] = load_weight(w2w, w2s, CLASSES, "w2_%d" % net)
+            nc.sync.dma_start(out=b2_raw[:, net, :], in_=b2.partition_broadcast(P))
+
+        def sort_biases(net):
+            b1_sorted[net] = keep.tile([P, D_H], F32, name="b1_sorted_%d" % net)
+            nc.vector.tensor_copy(
+                out=b1_sorted[net][:].rearrange("t (u p e) -> t u p e", u=2, e=2),
+                in_=b1_raw[net][:].rearrange("t (p u e) -> t u p e", u=2, e=2),
+            )
+            nc.vector.tensor_copy(out=b2_both[:, net, :], in_=b2_raw[:, net, :])
+
+        x_loaded, x_grouped, z_banks, pre_relu, h_grouped, h_packed = {}, {}, {}, {}, {}, {}
+        logit_banks, logits, neg_max, exp_f, scaled_o, coef_f = {}, {}, {}, {}, {}, {}
+
+        def load_x(job):
+            if 0 <= job < N_UNITS and job % UNITS_PER_LOAD == 0:
+                first = job * PAIR
+                x_rows = loads.tile([P, UNITS_PER_LOAD * PAIR, D_IN], BF16, name="x_rows")
+                nc.sync.dma_start(out=x_rows[:], in_=x_by_tile[:, first : first + UNITS_PER_LOAD * PAIR, :])
+                x_loaded[job // UNITS_PER_LOAD] = x_rows
+
+        def transpose_x(job):
+            if not 0 <= job < N_UNITS:
+                return
+            x_rows = x_loaded[job // UNITS_PER_LOAD]
+            words = x_rows[:].rearrange("p i k -> p (i k)").bitcast(F32)
+            words_per_tile = D_IN // 2
+            xt = psum_x.tile([P, PAIR, 2, P], F32, name="xt")
+            for j in range(PAIR):
+                start = ((job % UNITS_PER_LOAD) * PAIR + j) * words_per_tile
+                for u in range(2):
+                    nc.tensor.transpose(
+                        out=xt[:, j, u, :],
+                        in_=words[:, start + u : start + words_per_tile : 2],
+                        identity=identity[:],
+                    )
+            grouped = x_grouped_pool.tile([P, PAIR * P * PACK], BF16, name="x_grouped", align_bytes=64)
+            nc.scalar.copy(
+                out=grouped[:].bitcast(F32).rearrange("p (j w u) -> p j w u", j=PAIR, u=2),
+                in_=xt[:].rearrange("p j u w -> p j w u"),
+            )
+            x_grouped[job] = grouped
+
+        def quantise_x(job):
+            if not 0 <= job < N_UNITS:
+                return
+            cols = slice(job * PAIR * P, (job + 1) * PAIR * P)
+            nc.vector.quantize_mx(
+                out=x_words[:, cols].bitcast(FP8X4), scales=x_scales[:, cols], in_=x_grouped[job][:]
+            )
+
+        def layer1(job):
+            for net, unit in members(job):
+                for j in range(PAIR):
+                    cols = slice((unit * PAIR + j) * P, (unit * PAIR + j + 1) * P)
+                    z = psum_z.tile([P, D_H], F32, name="z")
+                    nc.tensor.matmul_mx(
+                        out=z[:],
+                        lhsT=x_words[:, cols].bitcast(FP8X4),
+                        lhsT_scale=x_scales[:, cols],
+                        rhs=w1_words[net][:].bitcast(FP8X4),
+                        rhs_scale=w1_scales[net][:],
+                        start=True,
+                        stop=True,
+                    )
+                    z_banks[(net, unit, j)] = z
+
+        def hidden_bias(job):
+            for net, unit in members(job):
+                pre = pre_pool.tile([P, PAIR, D_H], BF16, name="pre")
+                for j in range(PAIR):
+                    nc.vector.tensor_tensor(
+                        out=pre[:, j, :].rearrange("t (u p e) -> t u p e", u=2, e=2),
+                        in0=z_banks[(net, unit, j)][:].rearrange("t (p u e) -> t u p e", u=2, e=2),
+                        in1=b1_sorted[net][:].rearrange("t (u p e) -> t u p e", u=2, e=2),
+                        op=ALU.add,
+                    )
+                pre_relu[(net, unit)] = pre
+
+        def transpose_h(job):
+            for net, unit in members(job):
+                words = pre_relu[(net, unit)][:].bitcast(F32)
+                ht = psum_h.tile([P, PAIR, 2, P], F32, name="ht")
+                for j in range(PAIR):
+                    for u in range(2):
+                        nc.tensor.transpose(
+                            out=ht[:, j, u, :], in_=words[:, j, u * P : (u + 1) * P], identity=identity[:]
+                        )
+                grouped = h_grouped_pool.tile([P, PAIR, P * PACK], BF16, name="h_grouped", align_bytes=64)
+                for j in range(PAIR):
+                    nc.scalar.activation(
+                        out=grouped[:, j, :].rearrange("p (w u e) -> p w u e", u=2, e=2),
+                        in_=ht[:, j, :, :].bitcast(BF16).rearrange("p u (w e) -> p w u e", e=2),
+                        func=ACT.Relu,
+                    )
+                h_grouped[(net, unit)] = grouped
+
+        def quantise_h(job):
+            for net, unit in members(job):
+                h_words = h_packed_pool.tile([P, PAIR * P], U32, name="h_words", align_bytes=64)
+                h_scales = h_packed_pool.tile([P, PAIR * P], U8, name="h_scales", align_bytes=64)
+                nc.vector.quantize_mx(
+                    out=h_words[:].bitcast(FP8X4),
+                    scales=h_scales[:],
+                    in_=h_grouped[(net, unit)][:].rearrange("p j c -> p (j c)"),
+                )
+                h_packed[(net, unit)] = (h_words, h_scales)
+
+        def layer2(job):
+            if not members(job):
+                return
+            bank = psum_l.tile([P, 2, PAIR, CLASSES], F32, name="logit_bank")
+            for net, unit in members(job):
+                h_words, h_scales = h_packed[(net, unit)]
+                for j in range(PAIR):
+                    cols = slice(j * P, (j + 1) * P)
+                    nc.tensor.matmul_mx(
+                        out=bank[:, net, j, :],
+                        lhsT=h_words[:, cols].bitcast(FP8X4),
+                        lhsT_scale=h_scales[:, cols],
+                        rhs=w2_words[net][:].bitcast(FP8X4),
+                        rhs_scale=w2_scales[net][:],
+                        start=True,
+                        stop=True,
+                    )
+            logit_banks[job] = bank
+
+        def add_b2_and_find_max(job):
+            nets = [net for net, unit in members(job)]
+            if not nets:
+                return
+            some = slice(min(nets), max(nets) + 1)
+            zb = logit_pool.tile([P, 2, PAIR, CLASSES], F32, name="zb")
+            nc.vector.tensor_tensor(
+                out=zb[:, some, :, :],
+                in0=logit_banks[job][:, some, :, :],
+                in1=b2_both[:, some, :].unsqueeze(2).to_broadcast([P, len(nets), PAIR, CLASSES]),
+                op=ALU.add,
+            )
+            minus_max = logit_pool.tile([P, 2, PAIR], F32, name="minus_max")
+            nc.vector.tensor_reduce(
+                out=minus_max[:, some, :], in_=zb[:, some, :, :], axis=AXIS.X, op=ALU.max, negate=True
+            )
+            logits[job], neg_max[job] = zb, minus_max
+
+        def softmax_sums(job):
+            for net, unit in members(job):
+                if net == NET_F:
+                    exp_f[unit] = exp_f_pool.tile([P, PAIR, CLASSES], F32, name="exp_f")
+                for j in range(PAIR):
+                    i = unit * PAIR + j
+                    e = exp_o[:, i, :] if net == NET_O else exp_f[unit][:, j, :]
+                    total = sum_o if net == NET_O else sum_f
+                    nc.scalar.activation(
+                        out=e,
+                        in_=logits[job][:, net, j, :],
+                        func=ACT.Exp,
+                        bias=neg_max[job][:, net, j : j + 1],
+                        scale=1.0,
+                        accum_out=total[:, i : i + 1],
+                    )
+                    if net == NET_O:
+                        e2 = power_pool.tile([P, CLASSES], F32, name="e2")
+                        e4 = power_pool.tile([P, CLASSES], F32, name="e4")
+                        e8 = power_pool.tile([P, CLASSES], F32, name="e8")
+                        nc.scalar.activation(out=e2[:], in_=e, func=ACT.Square, accum_out=sum_o2[:, i : i + 1])
+                        nc.scalar.activation(out=e4[:], in_=e2[:], func=ACT.Square, accum_out=sum_o4[:, i : i + 1])
+                        nc.scalar.activation(out=e8[:], in_=e4[:], func=ACT.Square, accum_out=sum_o8[:, i : i + 1])
+
+        def gate_tile(name):
+            return gate_pool.tile([P, BLOCK_TILES], F32, name=name)
+
+        def times(name, a, b):
+            product = gate_tile(name)
+            nc.gpsimd.tensor_tensor(out=product[:], in0=a, in1=b, op=ALU.mult)
+            return product
+
+        def affine(name, a, scale, shift):
+            result = gate_tile(name)
+            nc.gpsimd.tensor_scalar(out=result[:], in0=a, scalar1=scale, scalar2=shift, op0=ALU.mult, op1=ALU.add)
+            return result
+
+        def inverse_series(v, two_over_m):
+            u = affine("u", v, -two_over_m, 1.0)
+            a = affine("a", u[:], 1.0, 1.0)
+            for doubling in range(3):
+                u = times("u", u[:], u[:])
+                one_plus = affine("one_plus", u[:], 1.0, 1.0)
+                a = times("a", a[:], one_plus[:])
+            return a
+
+        def gate(block):
+            cols = slice(block * BLOCK_TILES, (block + 1) * BLOCK_TILES)
+            nc.vector.reciprocal(out=inv_sum_o[:, cols], in_=sum_o[:, cols])
+            r1 = inv_sum_o[:, cols]
+            r2 = times("r2", r1, r1)
+            r4 = times("r4", r2[:], r2[:])
+            r8 = times("r8", r4[:], r4[:])
+            m2 = times("m2", sum_o2[:, cols], r2[:])
+            m4 = times("m4", sum_o4[:, cols], r4[:])
+            m8 = times("m8", sum_o8[:, cols], r8[:])
+            sm0 = affine("sm", m2[:], 1.0, TAU**2)
+            g0 = inverse_series(sm0[:], C0)
+            g0_squared = times("g0_squared", g0[:], g0[:])
+            scaled4 = affine("scaled", m4[:], C0**2, C0**2 * TAU**4)
+            sm1 = times("sm", scaled4[:], g0_squared[:])
+            g1 = inverse_series(sm1[:], 1.0)
+            factor = times("factor", g0_squared[:], g1[:])
+            factor_squared = times("factor_squared", factor[:], factor[:])
+            scaled8 = affine("scaled", m8[:], C0**4, C0**4 * TAU**8)
+            sm2 = times("sm", scaled8[:], factor_squared[:])
+            g2 = inverse_series(sm2[:], 1.0)
+            last = times("last", factor_squared[:], g2[:])
+            nc.gpsimd.tensor_scalar(
+                out=cond[:, cols], in0=last[:], scalar1=C0**4 * TAU**8, scalar2=0.0, op0=ALU.mult, op1=ALU.add
+            )
+            rest = affine("rest", cond[:, cols], -1.0, 1.0)
+            nc.gpsimd.tensor_tensor(out=coef_o[:, cols], in0=rest[:], in1=r1, op=ALU.mult)
+
+        def prepare_blend(job):
+            unit = job - LEAD
+            if not 0 <= unit < N_UNITS:
+                return
+            cols = slice(unit * PAIR, (unit + 1) * PAIR)
+            inv_sum_f = blend_pool.tile([P, PAIR], F32, name="inv_sum_f")
+            nc.vector.reciprocal(out=inv_sum_f[:], in_=sum_f[:, cols])
+            coef = blend_pool.tile([P, PAIR], F32, name="coef_f")
+            nc.vector.tensor_tensor(out=coef[:], in0=inv_sum_f[:], in1=cond[:, cols], op=ALU.mult)
+            part_o = blend_pool.tile([P, PAIR, CLASSES], F32, name="part_o")
+            for j in range(PAIR):
+                i = unit * PAIR + j
+                nc.scalar.activation(
+                    out=part_o[:, j, :], in_=exp_o[:, i, :], func=ACT.Copy, scale=coef_o[:, i : i + 1]
+                )
+            coef_f[unit], scaled_o[unit] = coef, part_o
+
+        def blend(job):
+            unit = job - LEAD
+            if not 0 <= unit < N_UNITS:
+                return
+            result = blend_pool.tile([P, PAIR, CLASSES], F32, name="result")
+            for j in range(PAIR):
+                nc.vector.scalar_tensor_tensor(
+                    out=result[:, j, :],
+                    in0=exp_f[unit][:, j, :],
+                    scalar=coef_f[unit][:, j : j + 1],
+                    in1=scaled_o[unit][:, j, :],
+                    op0=ALU.mult,
+                    op1=ALU.add,
+                )
+            nc.sync.dma_start(out=out_by_tile[:, unit * PAIR : (unit + 1) * PAIR, :], in_=result[:])
+
+        load_x(0)
+        load_network(NET_O)
+        load_x(UNITS_PER_LOAD)
+        load_network(NET_F)
+        sort_biases(NET_O)
+
+        for step in range(N_JOBS + AT_BLEND):
+            if step == LEAD:
+                sort_biases(NET_F)
+            load_x(step + LOAD_AHEAD)
+            quantise_h(step - AT_LAYER2)
+            quantise_x(step - AT_LAYER1)
+            layer2(step - AT_LAYER2)
+            layer1(step - AT_LAYER1)
+            blend(step - AT_BLEND)
+            prepare_blend(step - AT_PREPARE)
+            if (step - AT_GATE) % LEAD == LEAD - 1 and 0 <= step - AT_GATE < N_UNITS:
+                gate((step - AT_GATE) // LEAD)
+            softmax_sums(step - AT_SOFTMAX)
+            add_b2_and_find_max(step - AT_LAYER2)
+            hidden_bias(step - AT_LAYER1)
+            transpose_h(step - AT_TRANSPOSE_H)
+            transpose_x(step)

@@ -26,13 +26,17 @@ BLOCK_TILES = LEAD * PAIR
 UNITS_PER_LOAD = 2
 LOAD_AHEAD = 4
 
+AT_QUANTISE_X = 1
 AT_LAYER1 = 2
-AT_TRANSPOSE_H = 3
-AT_LAYER2 = 5
-AT_SOFTMAX = 6
-AT_GATE = 7
-AT_PREPARE = 12
-AT_BLEND = 13
+AT_HIDDEN_BIAS = 3
+AT_TRANSPOSE_H = 4
+AT_QUANTISE_H = 5
+AT_LAYER2 = 6
+AT_SOFTMAX = 7
+AT_GATE = 8
+AT_INVERT = 14
+AT_PREPARE = 15
+AT_BLEND = 16
 
 TAU = 0.5
 C0 = 2.0 / (2.0 + TAU * TAU)
@@ -68,9 +72,9 @@ def tile_combnethe_pa_t_kernel(
         x_grouped_pool = ctx.enter_context(tc.tile_pool(name="x_grouped", bufs=4))
         pre_pool = ctx.enter_context(tc.tile_pool(name="pre", bufs=6))
         h_grouped_pool = ctx.enter_context(tc.tile_pool(name="h_grouped", bufs=8))
-        h_packed_pool = ctx.enter_context(tc.tile_pool(name="h_packed", bufs=4))
+        h_packed_pool = ctx.enter_context(tc.tile_pool(name="h_packed", bufs=6))
         logit_pool = ctx.enter_context(tc.tile_pool(name="logit", bufs=3))
-        exp_f_pool = ctx.enter_context(tc.tile_pool(name="exp_f", bufs=9))
+        exp_f_pool = ctx.enter_context(tc.tile_pool(name="exp_f", bufs=11))
         power_pool = ctx.enter_context(tc.tile_pool(name="power", bufs=2))
         blend_pool = ctx.enter_context(tc.tile_pool(name="blend", bufs=4))
         gate_pool = ctx.enter_context(tc.tile_pool(name="gate", bufs=2))
@@ -129,7 +133,7 @@ def tile_combnethe_pa_t_kernel(
             nc.vector.tensor_copy(out=b2_both[:, net, :], in_=b2_raw[:, net, :])
 
         x_loaded, x_grouped, z_banks, pre_relu, h_grouped, h_packed = {}, {}, {}, {}, {}, {}
-        logit_banks, logits, neg_max, exp_f, scaled_o, coef_f = {}, {}, {}, {}, {}, {}
+        logit_banks, logits, neg_max, exp_f, inv_sum_f, scaled_o, coef_f = {}, {}, {}, {}, {}, {}, {}
 
         def load_x(job):
             if 0 <= job < N_UNITS and job % UNITS_PER_LOAD == 0:
@@ -244,23 +248,32 @@ def tile_combnethe_pa_t_kernel(
                     )
             logit_banks[job] = bank
 
-        def add_b2_and_find_max(job):
+        def networks_of(job):
             nets = [net for net, unit in members(job)]
-            if not nets:
+            return slice(min(nets), max(nets) + 1), len(nets)
+
+        def add_b2(job):
+            if not members(job):
                 return
-            some = slice(min(nets), max(nets) + 1)
+            some, n_nets = networks_of(job)
             zb = logit_pool.tile([P, 2, PAIR, CLASSES], F32, name="zb")
             nc.vector.tensor_tensor(
                 out=zb[:, some, :, :],
                 in0=logit_banks[job][:, some, :, :],
-                in1=b2_both[:, some, :].unsqueeze(2).to_broadcast([P, len(nets), PAIR, CLASSES]),
+                in1=b2_both[:, some, :].unsqueeze(2).to_broadcast([P, n_nets, PAIR, CLASSES]),
                 op=ALU.add,
             )
+            logits[job] = zb
+
+        def find_max(job):
+            if not members(job):
+                return
+            some, n_nets = networks_of(job)
             minus_max = logit_pool.tile([P, 2, PAIR], F32, name="minus_max")
             nc.vector.tensor_reduce(
-                out=minus_max[:, some, :], in_=zb[:, some, :, :], axis=AXIS.X, op=ALU.max, negate=True
+                out=minus_max[:, some, :], in_=logits[job][:, some, :, :], axis=AXIS.X, op=ALU.max, negate=True
             )
-            logits[job], neg_max[job] = zb, minus_max
+            neg_max[job] = minus_max
 
         def softmax_sums(job):
             for net, unit in members(job):
@@ -268,23 +281,28 @@ def tile_combnethe_pa_t_kernel(
                     exp_f[unit] = exp_f_pool.tile([P, PAIR, CLASSES], F32, name="exp_f")
                 for j in range(PAIR):
                     i = unit * PAIR + j
-                    e = exp_o[:, i, :] if net == NET_O else exp_f[unit][:, j, :]
-                    total = sum_o if net == NET_O else sum_f
                     nc.scalar.activation(
-                        out=e,
+                        out=exp_o[:, i, :] if net == NET_O else exp_f[unit][:, j, :],
                         in_=logits[job][:, net, j, :],
                         func=ACT.Exp,
                         bias=neg_max[job][:, net, j : j + 1],
                         scale=1.0,
-                        accum_out=total[:, i : i + 1],
+                        accum_out=(sum_o if net == NET_O else sum_f)[:, i : i + 1],
                     )
-                    if net == NET_O:
-                        e2 = power_pool.tile([P, CLASSES], F32, name="e2")
-                        e4 = power_pool.tile([P, CLASSES], F32, name="e4")
-                        e8 = power_pool.tile([P, CLASSES], F32, name="e8")
-                        nc.scalar.activation(out=e2[:], in_=e, func=ACT.Square, accum_out=sum_o2[:, i : i + 1])
-                        nc.scalar.activation(out=e4[:], in_=e2[:], func=ACT.Square, accum_out=sum_o4[:, i : i + 1])
-                        nc.scalar.activation(out=e8[:], in_=e4[:], func=ACT.Square, accum_out=sum_o8[:, i : i + 1])
+            if not 0 <= job < N_UNITS:
+                return
+            first = job * PAIR
+            power = exp_o[:, first : first + PAIR, :]
+            for sums in (sum_o2, sum_o4, sum_o8):
+                squared = power_pool.tile([P, PAIR, CLASSES], F32, name="squared")
+                for j in range(PAIR):
+                    nc.scalar.activation(
+                        out=squared[:, j, :],
+                        in_=power[:, j, :],
+                        func=ACT.Square,
+                        accum_out=sums[:, first + j : first + j + 1],
+                    )
+                power = squared
 
         def gate_tile(name):
             return gate_pool.tile([P, BLOCK_TILES], F32, name=name)
@@ -336,15 +354,21 @@ def tile_combnethe_pa_t_kernel(
             rest = affine("rest", cond[:, cols], -1.0, 1.0)
             nc.gpsimd.tensor_tensor(out=coef_o[:, cols], in0=rest[:], in1=r1, op=ALU.mult)
 
+        def invert_sum_f(job):
+            unit = job - LEAD
+            if not 0 <= unit < N_UNITS:
+                return
+            inverse = blend_pool.tile([P, PAIR], F32, name="inv_sum_f")
+            nc.vector.reciprocal(out=inverse[:], in_=sum_f[:, unit * PAIR : (unit + 1) * PAIR])
+            inv_sum_f[unit] = inverse
+
         def prepare_blend(job):
             unit = job - LEAD
             if not 0 <= unit < N_UNITS:
                 return
             cols = slice(unit * PAIR, (unit + 1) * PAIR)
-            inv_sum_f = blend_pool.tile([P, PAIR], F32, name="inv_sum_f")
-            nc.vector.reciprocal(out=inv_sum_f[:], in_=sum_f[:, cols])
             coef = blend_pool.tile([P, PAIR], F32, name="coef_f")
-            nc.vector.tensor_tensor(out=coef[:], in0=inv_sum_f[:], in1=cond[:, cols], op=ALU.mult)
+            nc.vector.tensor_tensor(out=coef[:], in0=inv_sum_f[unit][:], in1=cond[:, cols], op=ALU.mult)
             part_o = blend_pool.tile([P, PAIR, CLASSES], F32, name="part_o")
             for j in range(PAIR):
                 i = unit * PAIR + j
@@ -379,16 +403,18 @@ def tile_combnethe_pa_t_kernel(
             if step == LEAD:
                 sort_biases(NET_F)
             load_x(step + LOAD_AHEAD)
-            quantise_h(step - AT_LAYER2)
-            quantise_x(step - AT_LAYER1)
+            hidden_bias(step - AT_HIDDEN_BIAS)
             layer2(step - AT_LAYER2)
-            layer1(step - AT_LAYER1)
-            blend(step - AT_BLEND)
-            prepare_blend(step - AT_PREPARE)
-            if (step - AT_GATE) % LEAD == LEAD - 1 and 0 <= step - AT_GATE < N_UNITS:
-                gate((step - AT_GATE) // LEAD)
             softmax_sums(step - AT_SOFTMAX)
-            add_b2_and_find_max(step - AT_LAYER2)
-            hidden_bias(step - AT_LAYER1)
+            prepare_blend(step - AT_PREPARE)
             transpose_h(step - AT_TRANSPOSE_H)
             transpose_x(step)
+            layer1(step - AT_LAYER1)
+            add_b2(step - AT_LAYER2)
+            invert_sum_f(step - AT_INVERT)
+            quantise_h(step - AT_QUANTISE_H)
+            find_max(step - AT_LAYER2)
+            quantise_x(step - AT_QUANTISE_X)
+            blend(step - AT_BLEND)
+            if (step - AT_GATE) % LEAD == LEAD - 1 and 0 <= step - AT_GATE < N_UNITS:
+                gate((step - AT_GATE) // LEAD)

@@ -133,7 +133,7 @@ def tile_combnethe_pa_t_kernel(
             nc.vector.tensor_copy(out=b2_both[:, net, :], in_=b2_raw[:, net, :])
 
         x_loaded, x_grouped, z_banks, pre_relu, h_grouped, h_packed = {}, {}, {}, {}, {}, {}
-        logit_banks, logits, neg_max, exp_f, inv_sum_f, scaled_o, coef_f = {}, {}, {}, {}, {}, {}, {}
+        logit_banks, logits, neg_max, exp_f, inv_sum_f, coef_f = {}, {}, {}, {}, {}, {}
 
         def load_x(job):
             if 0 <= job < N_UNITS and job % UNITS_PER_LOAD == 0:
@@ -353,6 +353,15 @@ def tile_combnethe_pa_t_kernel(
             )
             rest = affine("rest", cond[:, cols], -1.0, 1.0)
             nc.gpsimd.tensor_tensor(out=coef_o[:, cols], in0=rest[:], in1=r1, op=ALU.mult)
+            for i in range(block * BLOCK_TILES, (block + 1) * BLOCK_TILES):
+                nc.gpsimd.tensor_scalar(
+                    out=exp_o[:, i, :],
+                    in0=exp_o[:, i, :],
+                    scalar1=coef_o[:, i : i + 1],
+                    scalar2=0.0,
+                    op0=ALU.mult,
+                    op1=ALU.add,
+                )
 
         def invert_sum_f(job):
             unit = job - LEAD
@@ -369,13 +378,7 @@ def tile_combnethe_pa_t_kernel(
             cols = slice(unit * PAIR, (unit + 1) * PAIR)
             coef = blend_pool.tile([P, PAIR], F32, name="coef_f")
             nc.vector.tensor_tensor(out=coef[:], in0=inv_sum_f[unit][:], in1=cond[:, cols], op=ALU.mult)
-            part_o = blend_pool.tile([P, PAIR, CLASSES], F32, name="part_o")
-            for j in range(PAIR):
-                i = unit * PAIR + j
-                nc.scalar.activation(
-                    out=part_o[:, j, :], in_=exp_o[:, i, :], func=ACT.Copy, scale=coef_o[:, i : i + 1]
-                )
-            coef_f[unit], scaled_o[unit] = coef, part_o
+            coef_f[unit] = coef
 
         def blend(job):
             unit = job - LEAD
@@ -387,7 +390,7 @@ def tile_combnethe_pa_t_kernel(
                     out=result[:, j, :],
                     in0=exp_f[unit][:, j, :],
                     scalar=coef_f[unit][:, j : j + 1],
-                    in1=scaled_o[unit][:, j, :],
+                    in1=exp_o[:, unit * PAIR + j, :],
                     op0=ALU.mult,
                     op1=ALU.add,
                 )

@@ -20,9 +20,10 @@ N_TILES = TOKENS // P
 PAIR = 2
 N_UNITS = N_TILES // PAIR
 NET_O, NET_F = 0, 1
-LEAD = 8
+LEAD = 12
 N_JOBS = N_UNITS + LEAD
-BLOCK_TILES = LEAD * PAIR
+GATE_UNITS = 8
+BLOCK_TILES = GATE_UNITS * PAIR
 UNITS_PER_LOAD = 2
 LOAD_AHEAD = 4
 
@@ -33,10 +34,11 @@ AT_TRANSPOSE_H = 4
 AT_QUANTISE_H = 5
 AT_LAYER2 = 6
 AT_SOFTMAX = 7
-AT_GATE = 8
-AT_INVERT = 14
-AT_PREPARE = 15
-AT_BLEND = 16
+AT_GATE = 7
+GATE_STEPS = 7
+AT_PREPARE = max(AT_SOFTMAX + 2, AT_GATE + GATE_UNITS - 1 + GATE_STEPS - LEAD)
+AT_INVERT = AT_PREPARE - 1
+AT_BLEND = AT_PREPARE + 1
 
 TAU = 0.5
 C0 = 2.0 / (2.0 + TAU * TAU)
@@ -74,7 +76,7 @@ def tile_combnethe_pa_t_kernel(
         h_grouped_pool = ctx.enter_context(tc.tile_pool(name="h_grouped", bufs=8))
         h_packed_pool = ctx.enter_context(tc.tile_pool(name="h_packed", bufs=6))
         logit_pool = ctx.enter_context(tc.tile_pool(name="logit", bufs=3))
-        exp_f_pool = ctx.enter_context(tc.tile_pool(name="exp_f", bufs=11))
+        exp_f_pool = ctx.enter_context(tc.tile_pool(name="exp_f", bufs=AT_BLEND - AT_SOFTMAX + 2))
         power_pool = ctx.enter_context(tc.tile_pool(name="power", bufs=2))
         blend_pool = ctx.enter_context(tc.tile_pool(name="blend", bufs=4))
         gate_pool = ctx.enter_context(tc.tile_pool(name="gate", bufs=2))
@@ -90,13 +92,15 @@ def tile_combnethe_pa_t_kernel(
         x_scales = keep.tile([P, TOKENS], U8, name="x_scales", align_bytes=64)
         exp_o = keep.tile([P, N_TILES, CLASSES], F32, name="exp_o")
         sum_o = keep.tile([P, N_TILES], F32, name="sum_o")
-        sum_o2 = keep.tile([P, N_TILES], F32, name="sum_o2")
-        sum_o4 = keep.tile([P, N_TILES], F32, name="sum_o4")
-        sum_o8 = keep.tile([P, N_TILES], F32, name="sum_o8")
+        sum_powers = keep.tile([P, 3, N_TILES], F32, name="sum_powers")
         sum_f = keep.tile([P, N_TILES], F32, name="sum_f")
         inv_sum_o = keep.tile([P, N_TILES], F32, name="inv_sum_o")
         cond = keep.tile([P, N_TILES], F32, name="cond")
         coef_o = keep.tile([P, N_TILES], F32, name="coef_o")
+
+        tau_powers = keep.tile([P, 3, BLOCK_TILES], F32, name="tau_powers")
+        for k in range(3):
+            nc.gpsimd.memset(tau_powers[:, k, :], TAU ** (2 ** (k + 1)))
 
         w1_words, w1_scales, w2_words, w2_scales = {}, {}, {}, {}
         b1_raw, b1_sorted = {}, {}
@@ -158,10 +162,11 @@ def tile_combnethe_pa_t_kernel(
                         identity=identity[:],
                     )
             grouped = x_grouped_pool.tile([P, PAIR * P * PACK], BF16, name="x_grouped", align_bytes=64)
-            nc.scalar.copy(
-                out=grouped[:].bitcast(F32).rearrange("p (j w u) -> p j w u", j=PAIR, u=2),
-                in_=xt[:].rearrange("p j u w -> p j w u"),
-            )
+            side_by_side = grouped[:].bitcast(F32).rearrange("p (j w u) -> p j w u", j=PAIR, u=2)
+            if job < LEAD:
+                nc.vector.tensor_copy(out=side_by_side, in_=xt[:].rearrange("p j u w -> p j w u"))
+            else:
+                nc.scalar.copy(out=side_by_side, in_=xt[:].rearrange("p j u w -> p j w u"))
             x_grouped[job] = grouped
 
         def quantise_x(job):
@@ -293,75 +298,68 @@ def tile_combnethe_pa_t_kernel(
                 return
             first = job * PAIR
             power = exp_o[:, first : first + PAIR, :]
-            for sums in (sum_o2, sum_o4, sum_o8):
+            for doubling in range(3):
                 squared = power_pool.tile([P, PAIR, CLASSES], F32, name="squared")
                 for j in range(PAIR):
                     nc.scalar.activation(
                         out=squared[:, j, :],
                         in_=power[:, j, :],
                         func=ACT.Square,
-                        accum_out=sums[:, first + j : first + j + 1],
+                        accum_out=sum_powers[:, doubling, first + j : first + j + 1],
                     )
                 power = squared
 
-        def gate_tile(name):
-            return gate_pool.tile([P, BLOCK_TILES], F32, name=name)
+        def times(out, a, b):
+            nc.gpsimd.tensor_tensor(out=out, in0=a, in1=b, op=ALU.mult)
 
-        def times(name, a, b):
-            product = gate_tile(name)
-            nc.gpsimd.tensor_tensor(out=product[:], in0=a, in1=b, op=ALU.mult)
-            return product
-
-        def affine(name, a, scale, shift):
-            result = gate_tile(name)
-            nc.gpsimd.tensor_scalar(out=result[:], in0=a, scalar1=scale, scalar2=shift, op0=ALU.mult, op1=ALU.add)
-            return result
+        def affine(out, a, scale, shift):
+            nc.gpsimd.tensor_scalar(out=out, in0=a, scalar1=scale, scalar2=shift, op0=ALU.mult, op1=ALU.add)
 
         def inverse_series(v, two_over_m):
-            u = affine("u", v, -two_over_m, 1.0)
-            a = affine("a", u[:], 1.0, 1.0)
-            for doubling in range(3):
-                u = times("u", u[:], u[:])
-                one_plus = affine("one_plus", u[:], 1.0, 1.0)
-                a = times("a", a[:], one_plus[:])
-            return a
+            powers = gate_pool.tile([P, 4, BLOCK_TILES], F32, name="powers")
+            affine(powers[:, 0, :], v, -two_over_m, 1.0)
+            for k in range(3):
+                times(powers[:, k + 1, :], powers[:, k, :], powers[:, k, :])
+            factors = gate_pool.tile([P, 4, BLOCK_TILES], F32, name="factors")
+            affine(factors[:], powers[:], 1.0, 1.0)
+            pairs = gate_pool.tile([P, 2, BLOCK_TILES], F32, name="pairs")
+            times(pairs[:], factors[:, 0:2, :], factors[:, 2:4, :])
+            series = gate_pool.tile([P, BLOCK_TILES], F32, name="series")
+            times(series[:], pairs[:, 0, :], pairs[:, 1, :])
+            return series
 
         def gate(block):
             cols = slice(block * BLOCK_TILES, (block + 1) * BLOCK_TILES)
             nc.vector.reciprocal(out=inv_sum_o[:, cols], in_=sum_o[:, cols])
             r1 = inv_sum_o[:, cols]
-            r2 = times("r2", r1, r1)
-            r4 = times("r4", r2[:], r2[:])
-            r8 = times("r8", r4[:], r4[:])
-            m2 = times("m2", sum_o2[:, cols], r2[:])
-            m4 = times("m4", sum_o4[:, cols], r4[:])
-            m8 = times("m8", sum_o8[:, cols], r8[:])
-            sm0 = affine("sm", m2[:], 1.0, TAU**2)
-            g0 = inverse_series(sm0[:], C0)
-            g0_squared = times("g0_squared", g0[:], g0[:])
-            scaled4 = affine("scaled", m4[:], C0**2, C0**2 * TAU**4)
-            sm1 = times("sm", scaled4[:], g0_squared[:])
-            g1 = inverse_series(sm1[:], 1.0)
-            factor = times("factor", g0_squared[:], g1[:])
-            factor_squared = times("factor_squared", factor[:], factor[:])
-            scaled8 = affine("scaled", m8[:], C0**4, C0**4 * TAU**8)
-            sm2 = times("sm", scaled8[:], factor_squared[:])
-            g2 = inverse_series(sm2[:], 1.0)
-            last = times("last", factor_squared[:], g2[:])
-            nc.gpsimd.tensor_scalar(
-                out=cond[:, cols], in0=last[:], scalar1=C0**4 * TAU**8, scalar2=0.0, op0=ALU.mult, op1=ALU.add
-            )
-            rest = affine("rest", cond[:, cols], -1.0, 1.0)
-            nc.gpsimd.tensor_tensor(out=coef_o[:, cols], in0=rest[:], in1=r1, op=ALU.mult)
+            r_powers = gate_pool.tile([P, 3, BLOCK_TILES], F32, name="r_powers")
+            times(r_powers[:, 0, :], r1, r1)
+            times(r_powers[:, 1, :], r_powers[:, 0, :], r_powers[:, 0, :])
+            times(r_powers[:, 2, :], r_powers[:, 1, :], r_powers[:, 1, :])
+            moments = gate_pool.tile([P, 3, BLOCK_TILES], F32, name="moments")
+            times(moments[:], sum_powers[:, :, cols], r_powers[:])
+            nc.gpsimd.tensor_tensor(out=moments[:], in0=moments[:], in1=tau_powers[:], op=ALU.add)
+            g0 = inverse_series(moments[:, 0, :], C0)
+            g0_squared = gate_pool.tile([P, BLOCK_TILES], F32, name="g0_squared")
+            times(g0_squared[:], g0[:], g0[:])
+            sm1 = gate_pool.tile([P, BLOCK_TILES], F32, name="sm1")
+            times(sm1[:], moments[:, 1, :], g0_squared[:])
+            g1 = inverse_series(sm1[:], C0**2)
+            factor = gate_pool.tile([P, BLOCK_TILES], F32, name="factor")
+            times(factor[:], g0_squared[:], g1[:])
+            factor_squared = gate_pool.tile([P, BLOCK_TILES], F32, name="factor_squared")
+            times(factor_squared[:], factor[:], factor[:])
+            sm2 = gate_pool.tile([P, BLOCK_TILES], F32, name="sm2")
+            times(sm2[:], moments[:, 2, :], factor_squared[:])
+            g2 = inverse_series(sm2[:], C0**4)
+            last = gate_pool.tile([P, BLOCK_TILES], F32, name="last")
+            times(last[:], factor_squared[:], g2[:])
+            affine(cond[:, cols], last[:], C0**4 * TAU**8, 0.0)
+            rest = gate_pool.tile([P, BLOCK_TILES], F32, name="rest")
+            affine(rest[:], cond[:, cols], -1.0, 1.0)
+            times(coef_o[:, cols], rest[:], r1)
             for i in range(block * BLOCK_TILES, (block + 1) * BLOCK_TILES):
-                nc.gpsimd.tensor_scalar(
-                    out=exp_o[:, i, :],
-                    in0=exp_o[:, i, :],
-                    scalar1=coef_o[:, i : i + 1],
-                    scalar2=0.0,
-                    op0=ALU.mult,
-                    op1=ALU.add,
-                )
+                affine(exp_o[:, i, :], exp_o[:, i, :], coef_o[:, i : i + 1], 0.0)
 
         def invert_sum_f(job):
             unit = job - LEAD
@@ -419,5 +417,5 @@ def tile_combnethe_pa_t_kernel(
             find_max(step - AT_LAYER2)
             quantise_x(step - AT_QUANTISE_X)
             blend(step - AT_BLEND)
-            if (step - AT_GATE) % LEAD == LEAD - 1 and 0 <= step - AT_GATE < N_UNITS:
-                gate((step - AT_GATE) // LEAD)
+            if (step - AT_GATE) % GATE_UNITS == GATE_UNITS - 1 and 0 <= step - AT_GATE < N_UNITS:
+                gate((step - AT_GATE) // GATE_UNITS)

@@ -17,28 +17,15 @@ P = 128
 PACK = 4
 TOKENS, D_IN, D_H, CLASSES = 8192, 512, 512, 128
 N_TILES = TOKENS // P
-PAIR = 2
-N_UNITS = N_TILES // PAIR
+GROUP = 4
+WIDE = GROUP * P
+N_GROUPS = N_TILES // GROUP
 NET_O, NET_F = 0, 1
-LEAD = 12
-N_JOBS = N_UNITS + LEAD
-GATE_UNITS = 8
-BLOCK_TILES = GATE_UNITS * PAIR
-UNITS_PER_LOAD = 2
-LOAD_AHEAD = 4
-
-AT_QUANTISE_X = 1
-AT_LAYER1 = 2
-AT_HIDDEN_BIAS = 3
-AT_TRANSPOSE_H = 4
-AT_QUANTISE_H = 5
-AT_LAYER2 = 6
-AT_SOFTMAX = 7
-AT_GATE = 7
-GATE_STEPS = 7
-AT_PREPARE = max(AT_SOFTMAX + 2, AT_GATE + GATE_UNITS - 1 + GATE_STEPS - LEAD)
-AT_INVERT = AT_PREPARE - 1
-AT_BLEND = AT_PREPARE + 1
+LEAD = 5
+GATE_GROUPS = 4
+BLOCK_TILES = GATE_GROUPS * GROUP
+LOAD_AHEAD = 6
+GPSIMD_TILES = 0
 
 TAU = 0.5
 C0 = 2.0 / (2.0 + TAU * TAU)
@@ -46,13 +33,21 @@ C0 = 2.0 / (2.0 + TAU * TAU)
 FLOPS = 2 * 2 * TOKENS * (D_IN * D_H + D_H * CLASSES)
 
 
-def members(job):
-    found = []
-    if 0 <= job < N_UNITS:
-        found.append((NET_O, job))
-    if 0 <= job - LEAD < N_UNITS:
-        found.append((NET_F, job - LEAD))
-    return found
+def all_jobs():
+    jobs = []
+    for k in range(N_GROUPS + LEAD):
+        if k < N_GROUPS:
+            jobs.append((NET_O, k))
+        if k >= LEAD:
+            jobs.append((NET_F, k - LEAD))
+    return jobs
+
+
+JOBS = all_jobs()
+
+
+def job_at(index):
+    return JOBS[index] if 0 <= index < len(JOBS) else (None, None)
 
 
 def tile_combnethe_pa_t_kernel(
@@ -70,20 +65,19 @@ def tile_combnethe_pa_t_kernel(
     with ExitStack() as ctx:
         ctx.enter_context(tc.manual_schedule())
         keep = ctx.enter_context(tc.tile_pool(name="keep", bufs=1))
-        loads = ctx.enter_context(tc.tile_pool(name="loads", bufs=4))
-        x_grouped_pool = ctx.enter_context(tc.tile_pool(name="x_grouped", bufs=4))
-        pre_pool = ctx.enter_context(tc.tile_pool(name="pre", bufs=6))
-        h_grouped_pool = ctx.enter_context(tc.tile_pool(name="h_grouped", bufs=8))
-        h_packed_pool = ctx.enter_context(tc.tile_pool(name="h_packed", bufs=6))
+        loads = ctx.enter_context(tc.tile_pool(name="loads", bufs=6))
+        x_grouped_pool = ctx.enter_context(tc.tile_pool(name="x_grouped", bufs=3))
+        h_pool = ctx.enter_context(tc.tile_pool(name="h", bufs=3))
+        h_grouped_pool = ctx.enter_context(tc.tile_pool(name="h_grouped", bufs=3))
+        h_packed_pool = ctx.enter_context(tc.tile_pool(name="h_packed", bufs=3))
         logit_pool = ctx.enter_context(tc.tile_pool(name="logit", bufs=3))
-        exp_f_pool = ctx.enter_context(tc.tile_pool(name="exp_f", bufs=AT_BLEND - AT_SOFTMAX + 2))
+        exp_f_pool = ctx.enter_context(tc.tile_pool(name="exp_f", bufs=3))
         power_pool = ctx.enter_context(tc.tile_pool(name="power", bufs=2))
-        blend_pool = ctx.enter_context(tc.tile_pool(name="blend", bufs=4))
+        blend_pool = ctx.enter_context(tc.tile_pool(name="blend", bufs=3))
         gate_pool = ctx.enter_context(tc.tile_pool(name="gate", bufs=2))
-        psum_x = ctx.enter_context(tc.psum_pool(name="psum_x", bufs=1))
+        psum_x = ctx.enter_context(tc.psum_pool(name="psum_x", bufs=2))
         psum_z = ctx.enter_context(tc.psum_pool(name="psum_z", bufs=4))
-        psum_h = ctx.enter_context(tc.psum_pool(name="psum_h", bufs=2))
-        psum_l = ctx.enter_context(tc.psum_pool(name="psum_l", bufs=1))
+        psum_l = ctx.enter_context(tc.psum_pool(name="psum_l", bufs=2))
 
         identity = keep.tile([P, P], F32, name="identity")
         make_identity(nc, identity[:])
@@ -102,8 +96,8 @@ def tile_combnethe_pa_t_kernel(
         for k in range(3):
             nc.gpsimd.memset(tau_powers[:, k, :], TAU ** (2 ** (k + 1)))
 
-        w1_words, w1_scales, w2_words, w2_scales = {}, {}, {}, {}
-        b1_raw, b1_sorted = {}, {}
+        w1_raw, w1_words, w1_scales, w2_words, w2_scales = {}, {}, {}, {}, {}
+        b1_raw, b1_col = {}, {}
         b2_raw = keep.tile([P, 2, CLASSES], BF16, name="b2_raw")
         b2_both = keep.tile([P, 2, CLASSES], F32, name="b2_both")
 
@@ -120,194 +114,218 @@ def tile_combnethe_pa_t_kernel(
                 )
             return words, scales
 
-        def load_network(net):
+        def load_layer1(net):
             w1w, w1s, b1, w2w, w2s, b2 = weights_in[net]
-            w1_words[net], w1_scales[net] = load_weight(w1w, w1s, D_H, "w1_%d" % net)
-            b1_raw[net] = keep.tile([P, D_H], BF16, name="b1_raw_%d" % net)
-            nc.sync.dma_start(out=b1_raw[net][:], in_=b1.partition_broadcast(P))
+            w1_raw[net] = load_weight(w1w, w1s, D_H, "w1_raw_%d" % net)
+            b1_raw[net] = keep.tile([P, PACK], BF16, name="b1_raw_%d" % net)
+            nc.sync.dma_start(out=b1_raw[net][:], in_=b1.rearrange("(p t) -> p t", t=PACK))
+
+        def load_layer2(net):
+            w1w, w1s, b1, w2w, w2s, b2 = weights_in[net]
             w2_words[net], w2_scales[net] = load_weight(w2w, w2s, CLASSES, "w2_%d" % net)
             nc.sync.dma_start(out=b2_raw[:, net, :], in_=b2.partition_broadcast(P))
 
-        def sort_biases(net):
-            b1_sorted[net] = keep.tile([P, D_H], F32, name="b1_sorted_%d" % net)
-            nc.vector.tensor_copy(
-                out=b1_sorted[net][:].rearrange("t (u p e) -> t u p e", u=2, e=2),
-                in_=b1_raw[net][:].rearrange("t (p u e) -> t u p e", u=2, e=2),
-            )
+        def sort_layer1(net):
+            engine = nc.vector if net == NET_O else nc.gpsimd
+            words, scales = w1_raw[net]
+            w1_words[net] = keep.tile([P, D_H], U32, name="w1_words_%d" % net, align_bytes=64)
+            w1_scales[net] = keep.tile([P, D_H], U8, name="w1_scales_%d" % net, align_bytes=64)
+            for sorted_tile, raw in ((w1_words[net], words), (w1_scales[net], scales)):
+                engine.tensor_copy(
+                    out=sorted_tile[:].rearrange("k (t p) -> k p t", t=PACK),
+                    in_=raw[:].rearrange("k (p t) -> k p t", t=PACK),
+                )
+            b1_col[net] = keep.tile([P, PACK], F32, name="b1_col_%d" % net)
+            engine.tensor_copy(out=b1_col[net][:], in_=b1_raw[net][:])
+
+        def widen_b2(net):
             nc.vector.tensor_copy(out=b2_both[:, net, :], in_=b2_raw[:, net, :])
 
-        x_loaded, x_grouped, z_banks, pre_relu, h_grouped, h_packed = {}, {}, {}, {}, {}, {}
-        logit_banks, logits, neg_max, exp_f, inv_sum_f, coef_f = {}, {}, {}, {}, {}, {}
+        x_loaded, x_banks, x_grouped, z_banks, hidden, h_grouped, h_packed = {}, {}, {}, {}, {}, {}, {}
+        logit_banks, logits, neg_max, exp_f = {}, {}, {}, {}
 
-        def load_x(job):
-            if 0 <= job < N_UNITS and job % UNITS_PER_LOAD == 0:
-                first = job * PAIR
-                x_rows = loads.tile([P, UNITS_PER_LOAD * PAIR, D_IN], BF16, name="x_rows")
-                nc.sync.dma_start(out=x_rows[:], in_=x_by_tile[:, first : first + UNITS_PER_LOAD * PAIR, :])
-                x_loaded[job // UNITS_PER_LOAD] = x_rows
-
-        def transpose_x(job):
-            if not 0 <= job < N_UNITS:
+        def load_x(g, pieces=1):
+            if not 0 <= g < N_GROUPS:
                 return
-            x_rows = x_loaded[job // UNITS_PER_LOAD]
-            words = x_rows[:].rearrange("p i k -> p (i k)").bitcast(F32)
+            x_rows = loads.tile([P, GROUP, D_IN], BF16, name="x_rows")
+            n = GROUP // pieces
+            for j in range(0, GROUP, n):
+                nc.sync.dma_start(
+                    out=x_rows[:, j : j + n, :], in_=x_by_tile[:, g * GROUP + j : g * GROUP + j + n, :]
+                )
+            x_loaded[g] = x_rows
+
+        def transpose_x(index):
+            net, g = job_at(index)
+            if net != NET_O:
+                return
+            words = x_loaded[g][:].rearrange("p i k -> p (i k)").bitcast(F32)
             words_per_tile = D_IN // 2
-            xt = psum_x.tile([P, PAIR, 2, P], F32, name="xt")
-            for j in range(PAIR):
-                start = ((job % UNITS_PER_LOAD) * PAIR + j) * words_per_tile
-                for u in range(2):
-                    nc.tensor.transpose(
-                        out=xt[:, j, u, :],
-                        in_=words[:, start + u : start + words_per_tile : 2],
-                        identity=identity[:],
-                    )
-            grouped = x_grouped_pool.tile([P, PAIR * P * PACK], BF16, name="x_grouped", align_bytes=64)
-            side_by_side = grouped[:].bitcast(F32).rearrange("p (j w u) -> p j w u", j=PAIR, u=2)
-            if job < LEAD:
-                nc.vector.tensor_copy(out=side_by_side, in_=xt[:].rearrange("p j u w -> p j w u"))
-            else:
-                nc.scalar.copy(out=side_by_side, in_=xt[:].rearrange("p j u w -> p j w u"))
-            x_grouped[job] = grouped
-
-        def quantise_x(job):
-            if not 0 <= job < N_UNITS:
-                return
-            cols = slice(job * PAIR * P, (job + 1) * PAIR * P)
-            nc.vector.quantize_mx(
-                out=x_words[:, cols].bitcast(FP8X4), scales=x_scales[:, cols], in_=x_grouped[job][:]
-            )
-
-        def layer1(job):
-            for net, unit in members(job):
-                for j in range(PAIR):
-                    cols = slice((unit * PAIR + j) * P, (unit * PAIR + j + 1) * P)
-                    z = psum_z.tile([P, D_H], F32, name="z")
-                    nc.tensor.matmul_mx(
-                        out=z[:],
-                        lhsT=x_words[:, cols].bitcast(FP8X4),
-                        lhsT_scale=x_scales[:, cols],
-                        rhs=w1_words[net][:].bitcast(FP8X4),
-                        rhs_scale=w1_scales[net][:],
-                        start=True,
-                        stop=True,
-                    )
-                    z_banks[(net, unit, j)] = z
-
-        def hidden_bias(job):
-            for net, unit in members(job):
-                pre = pre_pool.tile([P, PAIR, D_H], BF16, name="pre")
-                for j in range(PAIR):
-                    nc.vector.tensor_tensor(
-                        out=pre[:, j, :].rearrange("t (u p e) -> t u p e", u=2, e=2),
-                        in0=z_banks[(net, unit, j)][:].rearrange("t (p u e) -> t u p e", u=2, e=2),
-                        in1=b1_sorted[net][:].rearrange("t (u p e) -> t u p e", u=2, e=2),
-                        op=ALU.add,
-                    )
-                pre_relu[(net, unit)] = pre
-
-        def transpose_h(job):
-            for net, unit in members(job):
-                words = pre_relu[(net, unit)][:].bitcast(F32)
-                ht = psum_h.tile([P, PAIR, 2, P], F32, name="ht")
-                for j in range(PAIR):
+            for half in range(2):
+                xt = psum_x.tile([P, 2, 2, P], F32, name="xt")
+                for j in range(2):
+                    start = (half * 2 + j) * words_per_tile
                     for u in range(2):
                         nc.tensor.transpose(
-                            out=ht[:, j, u, :], in_=words[:, j, u * P : (u + 1) * P], identity=identity[:]
+                            out=xt[:, j, u, :],
+                            in_=words[:, start + u : start + words_per_tile : 2],
+                            identity=identity[:],
                         )
-                grouped = h_grouped_pool.tile([P, PAIR, P * PACK], BF16, name="h_grouped", align_bytes=64)
-                for j in range(PAIR):
-                    nc.scalar.activation(
-                        out=grouped[:, j, :].rearrange("p (w u e) -> p w u e", u=2, e=2),
-                        in_=ht[:, j, :, :].bitcast(BF16).rearrange("p u (w e) -> p w u e", e=2),
-                        func=ACT.Relu,
-                    )
-                h_grouped[(net, unit)] = grouped
+                x_banks[(g, half)] = xt
 
-        def quantise_h(job):
-            for net, unit in members(job):
-                h_words = h_packed_pool.tile([P, PAIR * P], U32, name="h_words", align_bytes=64)
-                h_scales = h_packed_pool.tile([P, PAIR * P], U8, name="h_scales", align_bytes=64)
-                nc.vector.quantize_mx(
-                    out=h_words[:].bitcast(FP8X4),
-                    scales=h_scales[:],
-                    in_=h_grouped[(net, unit)][:].rearrange("p j c -> p (j c)"),
+        def copy_x(index):
+            net, g = job_at(index)
+            if net != NET_O:
+                return
+            grouped = x_grouped_pool.tile([P, WIDE * PACK], BF16, name="x_grouped", align_bytes=64)
+            side_by_side = grouped[:].bitcast(F32).rearrange("p (h j w u) -> p h j w u", h=2, j=2, u=2)
+            for half in range(2):
+                nc.vector.tensor_copy(
+                    out=side_by_side[:, half, :, :, :], in_=x_banks[(g, half)][:].rearrange("p j u w -> p j w u")
                 )
-                h_packed[(net, unit)] = (h_words, h_scales)
+            x_grouped[g] = grouped
 
-        def layer2(job):
-            if not members(job):
+        def quantise_x(index):
+            net, g = job_at(index)
+            if net != NET_O:
                 return
-            bank = psum_l.tile([P, 2, PAIR, CLASSES], F32, name="logit_bank")
-            for net, unit in members(job):
-                h_words, h_scales = h_packed[(net, unit)]
-                for j in range(PAIR):
-                    cols = slice(j * P, (j + 1) * P)
-                    nc.tensor.matmul_mx(
-                        out=bank[:, net, j, :],
-                        lhsT=h_words[:, cols].bitcast(FP8X4),
-                        lhsT_scale=h_scales[:, cols],
-                        rhs=w2_words[net][:].bitcast(FP8X4),
-                        rhs_scale=w2_scales[net][:],
-                        start=True,
-                        stop=True,
-                    )
-            logit_banks[job] = bank
+            cols = slice(g * WIDE, (g + 1) * WIDE)
+            nc.vector.quantize_mx(
+                out=x_words[:, cols].bitcast(FP8X4), scales=x_scales[:, cols], in_=x_grouped[g][:]
+            )
 
-        def networks_of(job):
-            nets = [net for net, unit in members(job)]
-            return slice(min(nets), max(nets) + 1), len(nets)
-
-        def add_b2(job):
-            if not members(job):
+        def layer1(index):
+            net, g = job_at(index)
+            if net is None:
                 return
-            some, n_nets = networks_of(job)
-            zb = logit_pool.tile([P, 2, PAIR, CLASSES], F32, name="zb")
+            cols = slice(g * WIDE, (g + 1) * WIDE)
+            for t in range(PACK):
+                units = slice(t * P, (t + 1) * P)
+                z = psum_z.tile([P, WIDE], F32, name="z")
+                nc.tensor.matmul_mx(
+                    out=z[:],
+                    lhsT=w1_words[net][:, units].bitcast(FP8X4),
+                    lhsT_scale=w1_scales[net][:, units],
+                    rhs=x_words[:, cols].bitcast(FP8X4),
+                    rhs_scale=x_scales[:, cols],
+                    start=True,
+                    stop=True,
+                )
+                z_banks[(net, g, t)] = z
+
+        def relu(index):
+            net, g = job_at(index)
+            if net is None:
+                return
+            h = h_pool.tile([P, PACK, WIDE], BF16, name="h")
+            for t in range(PACK):
+                nc.scalar.activation(
+                    out=h[:, t, :], in_=z_banks[(net, g, t)][:], func=ACT.Relu, bias=b1_col[net][:, t : t + 1], scale=1.0
+                )
+            hidden[(net, g)] = h
+
+        def interleave(index):
+            net, g = job_at(index)
+            if net is None:
+                return
+            h = hidden[(net, g)]
+            grouped = h_grouped_pool.tile([P, WIDE, PACK], BF16, name="h_grouped", align_bytes=64)
+            split = GPSIMD_TILES * P
+            for j in range(GPSIMD_TILES):
+                cols = slice(j * P, (j + 1) * P)
+                nc.gpsimd.tensor_scalar(
+                    out=grouped[:, cols, :], in0=h[:, :, cols].rearrange("p t n -> p n t"),
+                    scalar1=1.0, scalar2=0.0, op0=ALU.mult, op1=ALU.add,
+                )
+            nc.vector.tensor_copy(out=grouped[:, split:, :], in_=h[:, :, split:].rearrange("p t n -> p n t"))
+            h_grouped[(net, g)] = grouped
+
+        def quantise_h(index):
+            net, g = job_at(index)
+            if net is None:
+                return
+            h_words = h_packed_pool.tile([P, WIDE], U32, name="h_words", align_bytes=64)
+            h_scales = h_packed_pool.tile([P, WIDE], U8, name="h_scales", align_bytes=64)
+            nc.vector.quantize_mx(
+                out=h_words[:].bitcast(FP8X4),
+                scales=h_scales[:],
+                in_=h_grouped[(net, g)][:].rearrange("p n t -> p (n t)"),
+            )
+            h_packed[(net, g)] = (h_words, h_scales)
+
+        def layer2(index):
+            net, g = job_at(index)
+            if net is None:
+                return
+            bank = psum_l.tile([P, GROUP, CLASSES], F32, name="logit_bank")
+            h_words, h_scales = h_packed[(net, g)]
+            for j in range(GROUP):
+                cols = slice(j * P, (j + 1) * P)
+                nc.tensor.matmul_mx(
+                    out=bank[:, j, :],
+                    lhsT=h_words[:, cols].bitcast(FP8X4),
+                    lhsT_scale=h_scales[:, cols],
+                    rhs=w2_words[net][:].bitcast(FP8X4),
+                    rhs_scale=w2_scales[net][:],
+                    start=True,
+                    stop=True,
+                )
+            logit_banks[(net, g)] = bank
+
+        def add_b2(index):
+            net, g = job_at(index)
+            if net is None:
+                return
+            zb = logit_pool.tile([P, GROUP, CLASSES], F32, name="zb")
             nc.vector.tensor_tensor(
-                out=zb[:, some, :, :],
-                in0=logit_banks[job][:, some, :, :],
-                in1=b2_both[:, some, :].unsqueeze(2).to_broadcast([P, n_nets, PAIR, CLASSES]),
+                out=zb[:],
+                in0=logit_banks[(net, g)][:],
+                in1=b2_both[:, net, :].unsqueeze(1).to_broadcast([P, GROUP, CLASSES]),
                 op=ALU.add,
             )
-            logits[job] = zb
+            logits[(net, g)] = zb
 
-        def find_max(job):
-            if not members(job):
+        def find_max(index):
+            net, g = job_at(index)
+            if net is None:
                 return
-            some, n_nets = networks_of(job)
-            minus_max = logit_pool.tile([P, 2, PAIR], F32, name="minus_max")
-            nc.vector.tensor_reduce(
-                out=minus_max[:, some, :], in_=logits[job][:, some, :, :], axis=AXIS.X, op=ALU.max, negate=True
-            )
-            neg_max[job] = minus_max
+            minus_max = logit_pool.tile([P, GROUP], F32, name="minus_max")
+            nc.vector.tensor_reduce(out=minus_max[:], in_=logits[(net, g)][:], axis=AXIS.X, op=ALU.max, negate=True)
+            neg_max[(net, g)] = minus_max
 
-        def softmax_sums(job):
-            for net, unit in members(job):
-                if net == NET_F:
-                    exp_f[unit] = exp_f_pool.tile([P, PAIR, CLASSES], F32, name="exp_f")
-                for j in range(PAIR):
-                    i = unit * PAIR + j
-                    nc.scalar.activation(
-                        out=exp_o[:, i, :] if net == NET_O else exp_f[unit][:, j, :],
-                        in_=logits[job][:, net, j, :],
-                        func=ACT.Exp,
-                        bias=neg_max[job][:, net, j : j + 1],
-                        scale=1.0,
-                        accum_out=(sum_o if net == NET_O else sum_f)[:, i : i + 1],
-                    )
-            if not 0 <= job < N_UNITS:
+        def exponentials(index):
+            net, g = job_at(index)
+            if net is None:
                 return
-            first = job * PAIR
-            power = exp_o[:, first : first + PAIR, :]
+            if net == NET_F:
+                exp_f[g] = exp_f_pool.tile([P, GROUP, CLASSES], F32, name="exp_f")
+            for j in range(GROUP):
+                i = g * GROUP + j
+                nc.scalar.activation(
+                    out=exp_o[:, i, :] if net == NET_O else exp_f[g][:, j, :],
+                    in_=logits[(net, g)][:, j, :],
+                    func=ACT.Exp,
+                    bias=neg_max[(net, g)][:, j : j + 1],
+                    scale=1.0,
+                    accum_out=(sum_o if net == NET_O else sum_f)[:, i : i + 1],
+                )
+
+        def powers(index, tiles):
+            net, g = job_at(index)
+            if net != NET_O:
+                return
+            source = exp_o[:, g * GROUP : (g + 1) * GROUP, :]
             for doubling in range(3):
-                squared = power_pool.tile([P, PAIR, CLASSES], F32, name="squared")
-                for j in range(PAIR):
+                squared = power_pool.tile([P, GROUP, CLASSES], F32, name="squared")
+                for j in tiles:
+                    i = g * GROUP + j
                     nc.scalar.activation(
                         out=squared[:, j, :],
-                        in_=power[:, j, :],
+                        in_=source[:, j, :],
                         func=ACT.Square,
-                        accum_out=sum_powers[:, doubling, first + j : first + j + 1],
+                        accum_out=sum_powers[:, doubling, i : i + 1],
                     )
-                power = squared
+                source = squared
 
         def times(out, a, b):
             nc.gpsimd.tensor_tensor(out=out, in0=a, in1=b, op=ALU.mult)
@@ -361,61 +379,78 @@ def tile_combnethe_pa_t_kernel(
             for i in range(block * BLOCK_TILES, (block + 1) * BLOCK_TILES):
                 affine(exp_o[:, i, :], exp_o[:, i, :], coef_o[:, i : i + 1], 0.0)
 
-        def invert_sum_f(job):
-            unit = job - LEAD
-            if not 0 <= unit < N_UNITS:
-                return
-            inverse = blend_pool.tile([P, PAIR], F32, name="inv_sum_f")
-            nc.vector.reciprocal(out=inverse[:], in_=sum_f[:, unit * PAIR : (unit + 1) * PAIR])
-            inv_sum_f[unit] = inverse
+        def gate_after(index):
+            net, g = job_at(index)
+            if net == NET_O and g % GATE_GROUPS == GATE_GROUPS - 1:
+                gate(g // GATE_GROUPS)
 
-        def prepare_blend(job):
-            unit = job - LEAD
-            if not 0 <= unit < N_UNITS:
-                return
-            cols = slice(unit * PAIR, (unit + 1) * PAIR)
-            coef = blend_pool.tile([P, PAIR], F32, name="coef_f")
-            nc.vector.tensor_tensor(out=coef[:], in0=inv_sum_f[unit][:], in1=cond[:, cols], op=ALU.mult)
-            coef_f[unit] = coef
+        inv_sum_f, coef_f = {}, {}
 
-        def blend(job):
-            unit = job - LEAD
-            if not 0 <= unit < N_UNITS:
+        def invert_sum_f(index):
+            net, g = job_at(index)
+            if net != NET_F:
                 return
-            result = blend_pool.tile([P, PAIR, CLASSES], F32, name="result")
-            for j in range(PAIR):
+            inverse = blend_pool.tile([P, GROUP], F32, name="inv_sum_f")
+            nc.vector.reciprocal(out=inverse[:], in_=sum_f[:, g * GROUP : (g + 1) * GROUP])
+            inv_sum_f[g] = inverse
+
+        def prepare_blend(index):
+            net, g = job_at(index)
+            if net != NET_F:
+                return
+            coef = blend_pool.tile([P, GROUP], F32, name="coef_f")
+            nc.vector.tensor_tensor(
+                out=coef[:], in0=inv_sum_f[g][:], in1=cond[:, g * GROUP : (g + 1) * GROUP], op=ALU.mult
+            )
+            coef_f[g] = coef
+
+        def blend(index):
+            net, g = job_at(index)
+            if net != NET_F:
+                return
+            result = blend_pool.tile([P, GROUP, CLASSES], F32, name="result")
+            for j in range(GROUP):
                 nc.vector.scalar_tensor_tensor(
                     out=result[:, j, :],
-                    in0=exp_f[unit][:, j, :],
-                    scalar=coef_f[unit][:, j : j + 1],
-                    in1=exp_o[:, unit * PAIR + j, :],
+                    in0=exp_f[g][:, j, :],
+                    scalar=coef_f[g][:, j : j + 1],
+                    in1=exp_o[:, g * GROUP + j, :],
                     op0=ALU.mult,
                     op1=ALU.add,
                 )
-            nc.sync.dma_start(out=out_by_tile[:, unit * PAIR : (unit + 1) * PAIR, :], in_=result[:])
+            nc.sync.dma_start(out=out_by_tile[:, g * GROUP : (g + 1) * GROUP, :], in_=result[:])
 
-        load_x(0)
-        load_network(NET_O)
-        load_x(UNITS_PER_LOAD)
-        load_network(NET_F)
-        sort_biases(NET_O)
+        load_x(0, pieces=2)
+        load_layer1(NET_O)
+        load_x(1)
+        load_layer2(NET_O)
+        load_x(2)
+        load_layer1(NET_F)
+        load_layer2(NET_F)
 
-        for step in range(N_JOBS + AT_BLEND):
-            if step == LEAD:
-                sort_biases(NET_F)
-            load_x(step + LOAD_AHEAD)
-            hidden_bias(step - AT_HIDDEN_BIAS)
-            layer2(step - AT_LAYER2)
-            softmax_sums(step - AT_SOFTMAX)
-            prepare_blend(step - AT_PREPARE)
-            transpose_h(step - AT_TRANSPOSE_H)
-            transpose_x(step)
-            layer1(step - AT_LAYER1)
-            add_b2(step - AT_LAYER2)
-            invert_sum_f(step - AT_INVERT)
-            quantise_h(step - AT_QUANTISE_H)
-            find_max(step - AT_LAYER2)
-            quantise_x(step - AT_QUANTISE_X)
-            blend(step - AT_BLEND)
-            if (step - AT_GATE) % GATE_UNITS == GATE_UNITS - 1 and 0 <= step - AT_GATE < N_UNITS:
-                gate((step - AT_GATE) // GATE_UNITS)
+        for step in range(-3, len(JOBS) + 5):
+            if step == -1:
+                sort_layer1(NET_O)
+            if step == 0:
+                widen_b2(NET_O)
+                widen_b2(NET_F)
+                sort_layer1(NET_F)
+            if job_at(step + LOAD_AHEAD)[0] == NET_O:
+                load_x(job_at(step + LOAD_AHEAD)[1])
+            layer2(step - 2)
+            layer1(step)
+            copy_x(step + 2)
+            transpose_x(step + 3)
+            exponentials(step - 3)
+            powers(step - 3, (0, 1))
+            powers(step - 4, (2, 3))
+            relu(step)
+            invert_sum_f(step - 4)
+            interleave(step - 1)
+            prepare_blend(step - 4)
+            add_b2(step - 2)
+            quantise_x(step + 1)
+            quantise_h(step - 1)
+            find_max(step - 2)
+            blend(step - 4)
+            gate_after(step - 4)

@@ -21,7 +21,7 @@ GROUP = 4
 WIDE = GROUP * P
 N_GROUPS = N_TILES // GROUP
 NET_O, NET_F = 0, 1
-LEAD = 5
+LEAD = 8
 GATE_GROUPS = 4
 BLOCK_TILES = GATE_GROUPS * GROUP
 LOAD_AHEAD = 6

@@ -92,10 +92,6 @@ def tile_combnethe_pa_t_kernel(
         cond = keep.tile([P, N_TILES], F32, name="cond")
         coef_o = keep.tile([P, N_TILES], F32, name="coef_o")
 
-        tau_powers = keep.tile([P, 3, BLOCK_TILES], F32, name="tau_powers")
-        for k in range(3):
-            nc.gpsimd.memset(tau_powers[:, k, :], TAU ** (2 ** (k + 1)))
-
         w1_raw, w1_words, w1_scales, w2_words, w2_scales = {}, {}, {}, {}, {}
         b1_raw, b1_col = {}, {}
         b2_raw = keep.tile([P, 2, CLASSES], BF16, name="b2_raw")
@@ -180,7 +176,7 @@ def tile_combnethe_pa_t_kernel(
             grouped = x_grouped_pool.tile([P, WIDE * PACK], BF16, name="x_grouped", align_bytes=64)
             side_by_side = grouped[:].bitcast(F32).rearrange("p (h j w u) -> p h j w u", h=2, j=2, u=2)
             for half in range(2):
-                nc.vector.tensor_copy(
+                nc.scalar.copy(
                     out=side_by_side[:, half, :, :, :], in_=x_banks[(g, half)][:].rearrange("p j u w -> p j w u")
                 )
             x_grouped[g] = grouped
@@ -327,57 +323,77 @@ def tile_combnethe_pa_t_kernel(
                     )
                 source = squared
 
-        def times(out, a, b):
-            nc.gpsimd.tensor_tensor(out=out, in0=a, in1=b, op=ALU.mult)
+        pending = []
 
-        def affine(out, a, scale, shift):
-            nc.gpsimd.tensor_scalar(out=out, in0=a, scalar1=scale, scalar2=shift, op0=ALU.mult, op1=ALU.add)
-
-        def inverse_series(v, two_over_m):
-            powers = gate_pool.tile([P, 4, BLOCK_TILES], F32, name="powers")
-            affine(powers[:, 0, :], v, -two_over_m, 1.0)
-            for k in range(3):
-                times(powers[:, k + 1, :], powers[:, k, :], powers[:, k, :])
-            factors = gate_pool.tile([P, 4, BLOCK_TILES], F32, name="factors")
-            affine(factors[:], powers[:], 1.0, 1.0)
-            pairs = gate_pool.tile([P, 2, BLOCK_TILES], F32, name="pairs")
-            times(pairs[:], factors[:, 0:2, :], factors[:, 2:4, :])
-            series = gate_pool.tile([P, BLOCK_TILES], F32, name="series")
-            times(series[:], pairs[:, 0, :], pairs[:, 1, :])
-            return series
+        def tick():
+            if pending:
+                operation = pending[0]
+                pending.remove(operation)
+                operation()
 
         def gate(block):
             cols = slice(block * BLOCK_TILES, (block + 1) * BLOCK_TILES)
-            nc.vector.reciprocal(out=inv_sum_o[:, cols], in_=sum_o[:, cols])
+
+            def column(name):
+                return gate_pool.tile([P, BLOCK_TILES], F32, name=name)
+
+            def times(out, a, b):
+                pending.append(lambda: nc.vector.tensor_tensor(out=out, in0=a, in1=b, op=ALU.mult))
+
+            def affine(out, a, scale, shift):
+                pending.append(
+                    lambda: nc.vector.tensor_scalar(
+                        out=out, in0=a, scalar1=scale, scalar2=shift, op0=ALU.mult, op1=ALU.add
+                    )
+                )
+
+            def shifted_times(out, a, shift, b):
+                pending.append(
+                    lambda: nc.vector.scalar_tensor_tensor(
+                        out=out, in0=a, scalar=shift, in1=b, op0=ALU.add, op1=ALU.mult
+                    )
+                )
+
+            def series(tag, v, scale, shift):
+                u = [column("u%d_%s" % (k, tag)) for k in range(4)]
+                partial = [column("partial%d_%s" % (k, tag)) for k in range(3)]
+                result = column("series_" + tag)
+                affine(u[0][:], v, scale, shift)
+                affine(partial[0][:], v, scale, shift + 1.0)
+                for k in range(3):
+                    times(u[k + 1][:], u[k][:], u[k][:])
+                shifted_times(partial[1][:], u[1][:], 1.0, partial[0][:])
+                shifted_times(partial[2][:], u[2][:], 1.0, partial[1][:])
+                shifted_times(result[:], u[3][:], 1.0, partial[2][:])
+                return result
+
             r1 = inv_sum_o[:, cols]
+            pending.append(lambda: nc.vector.reciprocal(out=r1, in_=sum_o[:, cols]))
             r_powers = gate_pool.tile([P, 3, BLOCK_TILES], F32, name="r_powers")
             times(r_powers[:, 0, :], r1, r1)
             times(r_powers[:, 1, :], r_powers[:, 0, :], r_powers[:, 0, :])
             times(r_powers[:, 2, :], r_powers[:, 1, :], r_powers[:, 1, :])
             moments = gate_pool.tile([P, 3, BLOCK_TILES], F32, name="moments")
             times(moments[:], sum_powers[:, :, cols], r_powers[:])
-            nc.gpsimd.tensor_tensor(out=moments[:], in0=moments[:], in1=tau_powers[:], op=ALU.add)
-            g0 = inverse_series(moments[:, 0, :], C0)
-            g0_squared = gate_pool.tile([P, BLOCK_TILES], F32, name="g0_squared")
+            g0 = series("g0", moments[:, 0, :], -C0, 1.0 - C0 * TAU**2)
+            g0_squared = column("g0_squared")
             times(g0_squared[:], g0[:], g0[:])
-            sm1 = gate_pool.tile([P, BLOCK_TILES], F32, name="sm1")
-            times(sm1[:], moments[:, 1, :], g0_squared[:])
-            g1 = inverse_series(sm1[:], C0**2)
-            factor = gate_pool.tile([P, BLOCK_TILES], F32, name="factor")
+            sm1 = column("sm1")
+            shifted_times(sm1[:], moments[:, 1, :], TAU**4, g0_squared[:])
+            g1 = series("g1", sm1[:], -(C0**2), 1.0)
+            factor = column("factor")
             times(factor[:], g0_squared[:], g1[:])
-            factor_squared = gate_pool.tile([P, BLOCK_TILES], F32, name="factor_squared")
+            factor_squared = column("factor_squared")
             times(factor_squared[:], factor[:], factor[:])
-            sm2 = gate_pool.tile([P, BLOCK_TILES], F32, name="sm2")
-            times(sm2[:], moments[:, 2, :], factor_squared[:])
-            g2 = inverse_series(sm2[:], C0**4)
-            last = gate_pool.tile([P, BLOCK_TILES], F32, name="last")
+            sm2 = column("sm2")
+            shifted_times(sm2[:], moments[:, 2, :], TAU**8, factor_squared[:])
+            g2 = series("g2", sm2[:], -(C0**4), 1.0)
+            last = column("last")
             times(last[:], factor_squared[:], g2[:])
             affine(cond[:, cols], last[:], C0**4 * TAU**8, 0.0)
-            rest = gate_pool.tile([P, BLOCK_TILES], F32, name="rest")
-            affine(rest[:], cond[:, cols], -1.0, 1.0)
+            rest = column("rest")
+            affine(rest[:], last[:], -(C0**4) * TAU**8, 1.0)
             times(coef_o[:, cols], rest[:], r1)
-            for i in range(block * BLOCK_TILES, (block + 1) * BLOCK_TILES):
-                affine(exp_o[:, i, :], exp_o[:, i, :], coef_o[:, i : i + 1], 0.0)
 
         def gate_after(index):
             net, g = job_at(index)
@@ -409,12 +425,19 @@ def tile_combnethe_pa_t_kernel(
             if net != NET_F:
                 return
             result = blend_pool.tile([P, GROUP, CLASSES], F32, name="result")
+            share = blend_pool.tile([P, GROUP, CLASSES], F32, name="share")
+            for j in range(GROUP):
+                i = g * GROUP + j
+                nc.vector.tensor_scalar(
+                    out=share[:, j, :], in0=exp_o[:, i, :], scalar1=coef_o[:, i : i + 1], scalar2=None, op0=ALU.mult
+                )
+            tick()
             for j in range(GROUP):
                 nc.vector.scalar_tensor_tensor(
                     out=result[:, j, :],
                     in0=exp_f[g][:, j, :],
                     scalar=coef_f[g][:, j : j + 1],
-                    in1=exp_o[:, g * GROUP + j, :],
+                    in1=share[:, j, :],
                     op0=ALU.mult,
                     op1=ALU.add,
                 )
@@ -446,11 +469,18 @@ def tile_combnethe_pa_t_kernel(
             powers(step - 4, (2, 3))
             relu(step)
             invert_sum_f(step - 4)
+            tick()
             interleave(step - 1)
             prepare_blend(step - 4)
+            tick()
             add_b2(step - 2)
+            tick()
             quantise_x(step + 1)
+            tick()
             quantise_h(step - 1)
+            tick()
             find_max(step - 2)
+            tick()
             blend(step - 4)
+            tick()
             gate_after(step - 4)

@@ -21,8 +21,8 @@ GROUP = 4
 WIDE = GROUP * P
 N_GROUPS = N_TILES // GROUP
 NET_O, NET_F = 0, 1
-LEAD = 8
-GATE_GROUPS = 4
+LEAD = 12
+GATE_GROUPS = 8
 BLOCK_TILES = GATE_GROUPS * GROUP
 LOAD_AHEAD = 6
 GPSIMD_TILES = 0
@@ -71,8 +71,8 @@ def tile_combnethe_pa_t_kernel(
         h_grouped_pool = ctx.enter_context(tc.tile_pool(name="h_grouped", bufs=3))
         h_packed_pool = ctx.enter_context(tc.tile_pool(name="h_packed", bufs=3))
         logit_pool = ctx.enter_context(tc.tile_pool(name="logit", bufs=3))
+        exp_o4_pool = ctx.enter_context(tc.tile_pool(name="exp_o4", bufs=3))
         exp_f_pool = ctx.enter_context(tc.tile_pool(name="exp_f", bufs=3))
-        power_pool = ctx.enter_context(tc.tile_pool(name="power", bufs=2))
         blend_pool = ctx.enter_context(tc.tile_pool(name="blend", bufs=3))
         gate_pool = ctx.enter_context(tc.tile_pool(name="gate", bufs=2))
         psum_x = ctx.enter_context(tc.psum_pool(name="psum_x", bufs=2))
@@ -85,10 +85,9 @@ def tile_combnethe_pa_t_kernel(
         x_words = keep.tile([P, TOKENS], U32, name="x_words", align_bytes=64)
         x_scales = keep.tile([P, TOKENS], U8, name="x_scales", align_bytes=64)
         exp_o = keep.tile([P, N_TILES, CLASSES], F32, name="exp_o")
-        sum_o = keep.tile([P, N_TILES], F32, name="sum_o")
-        sum_powers = keep.tile([P, 3, N_TILES], F32, name="sum_powers")
+        stats_1 = keep.tile([P, N_TILES // 2, 6], F32, name="stats_1")
+        stats_4 = keep.tile([P, N_TILES // 2, 6], F32, name="stats_4")
         sum_f = keep.tile([P, N_TILES], F32, name="sum_f")
-        inv_sum_o = keep.tile([P, N_TILES], F32, name="inv_sum_o")
         cond = keep.tile([P, N_TILES], F32, name="cond")
         coef_o = keep.tile([P, N_TILES], F32, name="coef_o")
 
@@ -289,39 +288,64 @@ def tile_combnethe_pa_t_kernel(
             nc.vector.tensor_reduce(out=minus_max[:], in_=logits[(net, g)][:], axis=AXIS.X, op=ALU.max, negate=True)
             neg_max[(net, g)] = minus_max
 
-        def exponentials(index):
-            net, g = job_at(index)
-            if net is None:
-                return
-            if net == NET_F:
-                exp_f[g] = exp_f_pool.tile([P, GROUP, CLASSES], F32, name="exp_f")
-            for j in range(GROUP):
-                i = g * GROUP + j
-                nc.scalar.activation(
-                    out=exp_o[:, i, :] if net == NET_O else exp_f[g][:, j, :],
-                    in_=logits[(net, g)][:, j, :],
-                    func=ACT.Exp,
-                    bias=neg_max[(net, g)][:, j : j + 1],
-                    scale=1.0,
-                    accum_out=(sum_o if net == NET_O else sum_f)[:, i : i + 1],
-                )
+        exp_o4, neg_max4 = {}, {}
 
-        def powers(index, tiles):
+        def four_times_max(index):
             net, g = job_at(index)
             if net != NET_O:
                 return
-            source = exp_o[:, g * GROUP : (g + 1) * GROUP, :]
-            for doubling in range(3):
-                squared = power_pool.tile([P, GROUP, CLASSES], F32, name="squared")
-                for j in tiles:
+            minus_max4 = logit_pool.tile([P, GROUP], F32, name="minus_max4")
+            nc.vector.tensor_scalar(
+                out=minus_max4[:], in0=neg_max[(net, g)][:], scalar1=4.0, scalar2=None, op0=ALU.mult
+            )
+            neg_max4[g] = minus_max4
+
+        def exponentials(index):
+            net, g = job_at(index)
+            if net == NET_F:
+                exp_f[g] = exp_f_pool.tile([P, GROUP, CLASSES], F32, name="exp_f")
+                for j in range(GROUP):
                     i = g * GROUP + j
                     nc.scalar.activation(
-                        out=squared[:, j, :],
-                        in_=source[:, j, :],
-                        func=ACT.Square,
-                        accum_out=sum_powers[:, doubling, i : i + 1],
+                        out=exp_f[g][:, j, :],
+                        in_=logits[(net, g)][:, j, :],
+                        func=ACT.Exp,
+                        bias=neg_max[(net, g)][:, j : j + 1],
+                        scale=1.0,
+                        accum_out=sum_f[:, i : i + 1],
                     )
-                source = squared
+            if net == NET_O:
+                exp_o4[g] = exp_o4_pool.tile([P, GROUP, CLASSES], F32, name="exp_o4")
+                for j in range(GROUP):
+                    nc.scalar.activation(
+                        out=exp_o[:, g * GROUP + j, :],
+                        in_=logits[(net, g)][:, j, :],
+                        func=ACT.Exp,
+                        bias=neg_max[(net, g)][:, j : j + 1],
+                        scale=1.0,
+                    )
+                for j in range(GROUP):
+                    nc.scalar.activation(
+                        out=exp_o4[g][:, j, :],
+                        in_=logits[(net, g)][:, j, :],
+                        func=ACT.Exp,
+                        bias=neg_max4[g][:, j : j + 1],
+                        scale=4.0,
+                    )
+
+        def statistics(index):
+            net, g = job_at(index)
+            if net != NET_O:
+                return
+            for pair in range(GROUP // 2):
+                j = 2 * pair
+                i = g * GROUP + j
+                nc.vector.bn_stats(
+                    out=stats_1[:, i // 2, :], in_=exp_o[:, i : i + 2, :].rearrange("p j c -> p c j")
+                )
+                nc.vector.bn_stats(
+                    out=stats_4[:, i // 2, :], in_=exp_o4[g][:, j : j + 2, :].rearrange("p j c -> p c j")
+                )
 
         pending = []
 
@@ -333,6 +357,7 @@ def tile_combnethe_pa_t_kernel(
 
         def gate(block):
             cols = slice(block * BLOCK_TILES, (block + 1) * BLOCK_TILES)
+            n = float(CLASSES)
 
             def column(name):
                 return gate_pool.tile([P, BLOCK_TILES], F32, name=name)
@@ -367,33 +392,49 @@ def tile_combnethe_pa_t_kernel(
                 shifted_times(result[:], u[3][:], 1.0, partial[2][:])
                 return result
 
-            r1 = inv_sum_o[:, cols]
-            pending.append(lambda: nc.vector.reciprocal(out=r1, in_=sum_o[:, cols]))
-            r_powers = gate_pool.tile([P, 3, BLOCK_TILES], F32, name="r_powers")
-            times(r_powers[:, 0, :], r1, r1)
-            times(r_powers[:, 1, :], r_powers[:, 0, :], r_powers[:, 0, :])
-            times(r_powers[:, 2, :], r_powers[:, 1, :], r_powers[:, 1, :])
-            moments = gate_pool.tile([P, 3, BLOCK_TILES], F32, name="moments")
-            times(moments[:], sum_powers[:, :, cols], r_powers[:])
-            g0 = series("g0", moments[:, 0, :], -C0, 1.0 - C0 * TAU**2)
+            pairs = slice(block * BLOCK_TILES // 2, (block + 1) * BLOCK_TILES // 2)
+            by_tile_1 = stats_1[:, pairs, :].rearrange("p q (j s) -> p (q j) s", s=3)
+            by_tile_4 = stats_4[:, pairs, :].rearrange("p q (j s) -> p (q j) s", s=3)
+            mean_1, deviation_1 = by_tile_1[:, :, 1], by_tile_1[:, :, 2]
+            mean_4, deviation_4 = by_tile_4[:, :, 1], by_tile_4[:, :, 2]
+            r1, r2, r4, r8 = column("r1"), column("r2"), column("r4"), column("r8")
+            pending.append(lambda: nc.vector.reciprocal(out=r1[:], in_=mean_1))
+            times(r2[:], r1[:], r1[:])
+            times(r4[:], r2[:], r2[:])
+            spread_1 = column("spread_1")
+            times(spread_1[:], deviation_1, r2[:])
+            times(r8[:], r4[:], r4[:])
+            moment_4 = column("moment_4")
+            times(moment_4[:], mean_4, r4[:])
+            spread_4 = column("spread_4")
+            times(spread_4[:], deviation_4, r8[:])
+            moment_4_squared = column("moment_4_squared")
+            times(moment_4_squared[:], moment_4[:], moment_4[:])
+            moment_8 = column("moment_8")
+            pending.append(
+                lambda: nc.vector.scalar_tensor_tensor(
+                    out=moment_8[:], in0=moment_4_squared[:], scalar=n, in1=spread_4[:], op0=ALU.mult, op1=ALU.add
+                )
+            )
+            g0 = series("g0", spread_1[:], -C0 / n**2, 1.0 - C0 * (TAU**2 + 1.0 / n))
             g0_squared = column("g0_squared")
             times(g0_squared[:], g0[:], g0[:])
             sm1 = column("sm1")
-            shifted_times(sm1[:], moments[:, 1, :], TAU**4, g0_squared[:])
-            g1 = series("g1", sm1[:], -(C0**2), 1.0)
+            shifted_times(sm1[:], moment_4[:], TAU**4 * n**3, g0_squared[:])
+            g1 = series("g1", sm1[:], -(C0**2) / n**3, 1.0)
             factor = column("factor")
             times(factor[:], g0_squared[:], g1[:])
             factor_squared = column("factor_squared")
             times(factor_squared[:], factor[:], factor[:])
             sm2 = column("sm2")
-            shifted_times(sm2[:], moments[:, 2, :], TAU**8, factor_squared[:])
-            g2 = series("g2", sm2[:], -(C0**4), 1.0)
+            shifted_times(sm2[:], moment_8[:], TAU**8 * n**8, factor_squared[:])
+            g2 = series("g2", sm2[:], -(C0**4) / n**8, 1.0)
             last = column("last")
             times(last[:], factor_squared[:], g2[:])
             affine(cond[:, cols], last[:], C0**4 * TAU**8, 0.0)
             rest = column("rest")
-            affine(rest[:], last[:], -(C0**4) * TAU**8, 1.0)
-            times(coef_o[:, cols], rest[:], r1)
+            affine(rest[:], last[:], -(C0**4) * TAU**8 / n, 1.0 / n)
+            times(coef_o[:, cols], rest[:], r1[:])
 
         def gate_after(index):
             net, g = job_at(index)
@@ -420,24 +461,31 @@ def tile_combnethe_pa_t_kernel(
             )
             coef_f[g] = coef
 
+        shares = {}
+
+        def share_o(index):
+            net, g = job_at(index)
+            if net != NET_F:
+                return
+            share = blend_pool.tile([P, GROUP, CLASSES], F32, name="share")
+            for j in range(GROUP):
+                i = g * GROUP + j
+                nc.scalar.activation(
+                    out=share[:, j, :], in_=exp_o[:, i, :], func=ACT.Copy, scale=coef_o[:, i : i + 1]
+                )
+            shares[g] = share
+
         def blend(index):
             net, g = job_at(index)
             if net != NET_F:
                 return
             result = blend_pool.tile([P, GROUP, CLASSES], F32, name="result")
-            share = blend_pool.tile([P, GROUP, CLASSES], F32, name="share")
-            for j in range(GROUP):
-                i = g * GROUP + j
-                nc.vector.tensor_scalar(
-                    out=share[:, j, :], in0=exp_o[:, i, :], scalar1=coef_o[:, i : i + 1], scalar2=None, op0=ALU.mult
-                )
-            tick()
             for j in range(GROUP):
                 nc.vector.scalar_tensor_tensor(
                     out=result[:, j, :],
                     in0=exp_f[g][:, j, :],
                     scalar=coef_f[g][:, j : j + 1],
-                    in1=share[:, j, :],
+                    in1=shares[g][:, j, :],
                     op0=ALU.mult,
                     op1=ALU.add,
                 )
@@ -464,9 +512,8 @@ def tile_combnethe_pa_t_kernel(
             layer1(step)
             copy_x(step + 2)
             transpose_x(step + 3)
+            share_o(step - 4)
             exponentials(step - 3)
-            powers(step - 3, (0, 1))
-            powers(step - 4, (2, 3))
             relu(step)
             invert_sum_f(step - 4)
             tick()
@@ -475,6 +522,8 @@ def tile_combnethe_pa_t_kernel(
             tick()
             add_b2(step - 2)
             tick()
+            statistics(step - 4)
+            tick()
             quantise_x(step + 1)
             tick()
             quantise_h(step - 1)
@@ -482,5 +531,7 @@ def tile_combnethe_pa_t_kernel(
             find_max(step - 2)
             tick()
             blend(step - 4)
+            tick()
+            four_times_max(step - 2)
             tick()
             gate_after(step - 4)

@@ -24,7 +24,7 @@ NET_O, NET_F = 0, 1
 LEAD = 12
 GATE_GROUPS = 8
 BLOCK_TILES = GATE_GROUPS * GROUP
-LOAD_AHEAD = 6
+LOAD_AHEAD = 5
 GPSIMD_TILES = 0
 
 TAU = 0.5
@@ -232,7 +232,10 @@ def tile_combnethe_pa_t_kernel(
                     out=grouped[:, cols, :], in0=h[:, :, cols].rearrange("p t n -> p n t"),
                     scalar1=1.0, scalar2=0.0, op0=ALU.mult, op1=ALU.add,
                 )
-            nc.vector.tensor_copy(out=grouped[:, split:, :], in_=h[:, :, split:].rearrange("p t n -> p n t"))
+            nc.vector.tensor_copy(
+                out=grouped[:, split:, :].rearrange("p (c i) t -> p c t i", i=4),
+                in_=h[:, :, split:].rearrange("p t (c i) -> p c t i", i=4),
+            )
             h_grouped[(net, g)] = grouped
 
         def quantise_h(index):
@@ -499,19 +502,20 @@ def tile_combnethe_pa_t_kernel(
         load_layer1(NET_F)
         load_layer2(NET_F)
 
-        for step in range(-3, len(JOBS) + 5):
+        for step in range(-2, len(JOBS) + 5):
             if step == -1:
                 sort_layer1(NET_O)
             if step == 0:
+                sort_layer1(NET_F)
+            if step == 2:
                 widen_b2(NET_O)
                 widen_b2(NET_F)
-                sort_layer1(NET_F)
-            if job_at(step + LOAD_AHEAD)[0] == NET_O:
+            if step + LOAD_AHEAD > 2 and job_at(step + LOAD_AHEAD)[0] == NET_O:
                 load_x(job_at(step + LOAD_AHEAD)[1])
             layer2(step - 2)
             layer1(step)
-            copy_x(step + 2)
-            transpose_x(step + 3)
+            copy_x(step + 1)
+            transpose_x(step + 2)
             share_o(step - 4)
             exponentials(step - 3)
             relu(step)

@@ -21,26 +21,18 @@ GROUP = 4
 WIDE = GROUP * P
 N_GROUPS = N_TILES // GROUP
 NET_O, NET_F = 0, 1
-LEAD = 12
-GATE_GROUPS = 8
-BLOCK_TILES = GATE_GROUPS * GROUP
 LOAD_AHEAD = 5
-GPSIMD_TILES = 0
+FIRST_BLEND = 25
 
 TAU = 0.5
 C0 = 2.0 / (2.0 + TAU * TAU)
+COND_SCALE = C0**4 * TAU**8
 
 FLOPS = 2 * 2 * TOKENS * (D_IN * D_H + D_H * CLASSES)
 
 
 def all_jobs():
-    jobs = []
-    for k in range(N_GROUPS + LEAD):
-        if k < N_GROUPS:
-            jobs.append((NET_O, k))
-        if k >= LEAD:
-            jobs.append((NET_F, k - LEAD))
-    return jobs
+    return [(net, g) for net in (NET_O, NET_F) for g in range(N_GROUPS)]
 
 
 JOBS = all_jobs()
@@ -48,6 +40,12 @@ JOBS = all_jobs()
 
 def job_at(index):
     return JOBS[index] if 0 <= index < len(JOBS) else (None, None)
+
+
+def vector_x_banks(g):
+    if g == 1:
+        return (0, 1)
+    return (1,) if g == 0 else ()
 
 
 def tile_combnethe_pa_t_kernel(
@@ -72,9 +70,9 @@ def tile_combnethe_pa_t_kernel(
         h_packed_pool = ctx.enter_context(tc.tile_pool(name="h_packed", bufs=3))
         logit_pool = ctx.enter_context(tc.tile_pool(name="logit", bufs=3))
         exp_o4_pool = ctx.enter_context(tc.tile_pool(name="exp_o4", bufs=3))
-        exp_f_pool = ctx.enter_context(tc.tile_pool(name="exp_f", bufs=3))
+        exp_f_pool = ctx.enter_context(tc.tile_pool(name="exp_f", bufs=9))
         blend_pool = ctx.enter_context(tc.tile_pool(name="blend", bufs=3))
-        gate_pool = ctx.enter_context(tc.tile_pool(name="gate", bufs=2))
+        gate_pool = ctx.enter_context(tc.tile_pool(name="gate", bufs=1))
         psum_x = ctx.enter_context(tc.psum_pool(name="psum_x", bufs=2))
         psum_z = ctx.enter_context(tc.psum_pool(name="psum_z", bufs=4))
         psum_l = ctx.enter_context(tc.psum_pool(name="psum_l", bufs=2))
@@ -88,7 +86,7 @@ def tile_combnethe_pa_t_kernel(
         stats_1 = keep.tile([P, N_TILES // 2, 6], F32, name="stats_1")
         stats_4 = keep.tile([P, N_TILES // 2, 6], F32, name="stats_4")
         sum_f = keep.tile([P, N_TILES], F32, name="sum_f")
-        cond = keep.tile([P, N_TILES], F32, name="cond")
+        gate_last = keep.tile([P, N_TILES], F32, name="gate_last")
         coef_o = keep.tile([P, N_TILES], F32, name="coef_o")
 
         w1_raw, w1_words, w1_scales, w2_words, w2_scales = {}, {}, {}, {}, {}
@@ -121,17 +119,16 @@ def tile_combnethe_pa_t_kernel(
             nc.sync.dma_start(out=b2_raw[:, net, :], in_=b2.partition_broadcast(P))
 
         def sort_layer1(net):
-            engine = nc.vector if net == NET_O else nc.gpsimd
             words, scales = w1_raw[net]
             w1_words[net] = keep.tile([P, D_H], U32, name="w1_words_%d" % net, align_bytes=64)
             w1_scales[net] = keep.tile([P, D_H], U8, name="w1_scales_%d" % net, align_bytes=64)
             for sorted_tile, raw in ((w1_words[net], words), (w1_scales[net], scales)):
-                engine.tensor_copy(
-                    out=sorted_tile[:].rearrange("k (t p) -> k p t", t=PACK),
-                    in_=raw[:].rearrange("k (p t) -> k p t", t=PACK),
+                nc.vector.tensor_copy(
+                    out=sorted_tile[:].rearrange("k (t p) -> k t p", t=PACK),
+                    in_=raw[:].rearrange("k (p t) -> k t p", t=PACK),
                 )
             b1_col[net] = keep.tile([P, PACK], F32, name="b1_col_%d" % net)
-            engine.tensor_copy(out=b1_col[net][:], in_=b1_raw[net][:])
+            nc.vector.tensor_copy(out=b1_col[net][:], in_=b1_raw[net][:])
 
         def widen_b2(net):
             nc.vector.tensor_copy(out=b2_both[:, net, :], in_=b2_raw[:, net, :])
@@ -175,9 +172,8 @@ def tile_combnethe_pa_t_kernel(
             grouped = x_grouped_pool.tile([P, WIDE * PACK], BF16, name="x_grouped", align_bytes=64)
             side_by_side = grouped[:].bitcast(F32).rearrange("p (h j w u) -> p h j w u", h=2, j=2, u=2)
             for half in range(2):
-                nc.scalar.copy(
-                    out=side_by_side[:, half, :, :, :], in_=x_banks[(g, half)][:].rearrange("p j u w -> p j w u")
-                )
+                copy = nc.vector.tensor_copy if half in vector_x_banks(g) else nc.scalar.copy
+                copy(out=side_by_side[:, half, :, :, :], in_=x_banks[(g, half)][:].rearrange("p j u w -> p j w u"))
             x_grouped[g] = grouped
 
         def quantise_x(index):
@@ -214,9 +210,13 @@ def tile_combnethe_pa_t_kernel(
                 return
             h = h_pool.tile([P, PACK, WIDE], BF16, name="h")
             for t in range(PACK):
-                nc.scalar.activation(
-                    out=h[:, t, :], in_=z_banks[(net, g, t)][:], func=ACT.Relu, bias=b1_col[net][:, t : t + 1], scale=1.0
-                )
+                z, b1 = z_banks[(net, g, t)], b1_col[net][:, t : t + 1]
+                if index == 0 and t >= 2:
+                    nc.vector.tensor_scalar(
+                        out=h[:, t, :], in0=z[:], scalar1=b1, scalar2=0.0, op0=ALU.add, op1=ALU.max
+                    )
+                else:
+                    nc.scalar.activation(out=h[:, t, :], in_=z[:], func=ACT.Relu, bias=b1, scale=1.0)
             hidden[(net, g)] = h
 
         def interleave(index):
@@ -225,16 +225,9 @@ def tile_combnethe_pa_t_kernel(
                 return
             h = hidden[(net, g)]
             grouped = h_grouped_pool.tile([P, WIDE, PACK], BF16, name="h_grouped", align_bytes=64)
-            split = GPSIMD_TILES * P
-            for j in range(GPSIMD_TILES):
-                cols = slice(j * P, (j + 1) * P)
-                nc.gpsimd.tensor_scalar(
-                    out=grouped[:, cols, :], in0=h[:, :, cols].rearrange("p t n -> p n t"),
-                    scalar1=1.0, scalar2=0.0, op0=ALU.mult, op1=ALU.add,
-                )
             nc.vector.tensor_copy(
-                out=grouped[:, split:, :].rearrange("p (c i) t -> p c t i", i=4),
-                in_=h[:, :, split:].rearrange("p t (c i) -> p c t i", i=4),
+                out=grouped[:].rearrange("p (c i) t -> p c t i", i=4),
+                in_=h[:].rearrange("p t (c i) -> p c t i", i=4),
             )
             h_grouped[(net, g)] = grouped
 
@@ -298,9 +291,7 @@ def tile_combnethe_pa_t_kernel(
             if net != NET_O:
                 return
             minus_max4 = logit_pool.tile([P, GROUP], F32, name="minus_max4")
-            nc.vector.tensor_scalar(
-                out=minus_max4[:], in0=neg_max[(net, g)][:], scalar1=4.0, scalar2=None, op0=ALU.mult
-            )
+            nc.scalar.activation(out=minus_max4[:], in_=neg_max[(net, g)][:], func=ACT.Copy, scale=4.0)
             neg_max4[g] = minus_max4
 
         def exponentials(index):
@@ -358,12 +349,15 @@ def tile_combnethe_pa_t_kernel(
                 pending.remove(operation)
                 operation()
 
-        def gate(block):
-            cols = slice(block * BLOCK_TILES, (block + 1) * BLOCK_TILES)
+        def drain():
+            while pending:
+                tick()
+
+        def gate():
             n = float(CLASSES)
 
             def column(name):
-                return gate_pool.tile([P, BLOCK_TILES], F32, name=name)
+                return gate_pool.tile([P, N_TILES], F32, name=name)
 
             def times(out, a, b):
                 pending.append(lambda: nc.vector.tensor_tensor(out=out, in0=a, in1=b, op=ALU.mult))
@@ -395,9 +389,8 @@ def tile_combnethe_pa_t_kernel(
                 shifted_times(result[:], u[3][:], 1.0, partial[2][:])
                 return result
 
-            pairs = slice(block * BLOCK_TILES // 2, (block + 1) * BLOCK_TILES // 2)
-            by_tile_1 = stats_1[:, pairs, :].rearrange("p q (j s) -> p (q j) s", s=3)
-            by_tile_4 = stats_4[:, pairs, :].rearrange("p q (j s) -> p (q j) s", s=3)
+            by_tile_1 = stats_1[:].rearrange("p q (j s) -> p (q j) s", s=3)
+            by_tile_4 = stats_4[:].rearrange("p q (j s) -> p (q j) s", s=3)
             mean_1, deviation_1 = by_tile_1[:, :, 1], by_tile_1[:, :, 2]
             mean_4, deviation_4 = by_tile_4[:, :, 1], by_tile_4[:, :, 2]
             r1, r2, r4, r8 = column("r1"), column("r2"), column("r4"), column("r8")
@@ -432,44 +425,18 @@ def tile_combnethe_pa_t_kernel(
             sm2 = column("sm2")
             shifted_times(sm2[:], moment_8[:], TAU**8 * n**8, factor_squared[:])
             g2 = series("g2", sm2[:], -(C0**4) / n**8, 1.0)
-            last = column("last")
-            times(last[:], factor_squared[:], g2[:])
-            affine(cond[:, cols], last[:], C0**4 * TAU**8, 0.0)
+            times(gate_last[:], factor_squared[:], g2[:])
             rest = column("rest")
-            affine(rest[:], last[:], -(C0**4) * TAU**8 / n, 1.0 / n)
-            times(coef_o[:, cols], rest[:], r1[:])
+            affine(rest[:], gate_last[:], -COND_SCALE / n, 1.0 / n)
+            times(coef_o[:], rest[:], r1[:])
 
-        def gate_after(index):
-            net, g = job_at(index)
-            if net == NET_O and g % GATE_GROUPS == GATE_GROUPS - 1:
-                gate(g // GATE_GROUPS)
+        inv_sum_f, coef_f, shares = {}, {}, {}
 
-        inv_sum_f, coef_f = {}, {}
+        def blends_at(step):
+            first = len(JOBS) - N_GROUPS
+            return [g for g in range(N_GROUPS) if max(first + g + 4, FIRST_BLEND + g // 2) == step]
 
-        def invert_sum_f(index):
-            net, g = job_at(index)
-            if net != NET_F:
-                return
-            inverse = blend_pool.tile([P, GROUP], F32, name="inv_sum_f")
-            nc.vector.reciprocal(out=inverse[:], in_=sum_f[:, g * GROUP : (g + 1) * GROUP])
-            inv_sum_f[g] = inverse
-
-        def prepare_blend(index):
-            net, g = job_at(index)
-            if net != NET_F:
-                return
-            coef = blend_pool.tile([P, GROUP], F32, name="coef_f")
-            nc.vector.tensor_tensor(
-                out=coef[:], in0=inv_sum_f[g][:], in1=cond[:, g * GROUP : (g + 1) * GROUP], op=ALU.mult
-            )
-            coef_f[g] = coef
-
-        shares = {}
-
-        def share_o(index):
-            net, g = job_at(index)
-            if net != NET_F:
-                return
+        def share_o(g):
             share = blend_pool.tile([P, GROUP, CLASSES], F32, name="share")
             for j in range(GROUP):
                 i = g * GROUP + j
@@ -478,10 +445,24 @@ def tile_combnethe_pa_t_kernel(
                 )
             shares[g] = share
 
-        def blend(index):
-            net, g = job_at(index)
-            if net != NET_F:
-                return
+        def invert_sum_f(g):
+            inverse = blend_pool.tile([P, GROUP], F32, name="inv_sum_f")
+            nc.vector.reciprocal(out=inverse[:], in_=sum_f[:, g * GROUP : (g + 1) * GROUP])
+            inv_sum_f[g] = inverse
+
+        def prepare_blend(g):
+            coef = blend_pool.tile([P, GROUP], F32, name="coef_f")
+            nc.vector.scalar_tensor_tensor(
+                out=coef[:],
+                in0=inv_sum_f[g][:],
+                scalar=COND_SCALE,
+                in1=gate_last[:, g * GROUP : (g + 1) * GROUP],
+                op0=ALU.mult,
+                op1=ALU.mult,
+            )
+            coef_f[g] = coef
+
+        def blend(g):
             result = blend_pool.tile([P, GROUP, CLASSES], F32, name="result")
             for j in range(GROUP):
                 nc.vector.scalar_tensor_tensor(
@@ -502,27 +483,34 @@ def tile_combnethe_pa_t_kernel(
         load_layer1(NET_F)
         load_layer2(NET_F)
 
-        for step in range(-2, len(JOBS) + 5):
+        for step in range(-2, len(JOBS) + 4):
             if step == -1:
                 sort_layer1(NET_O)
-            if step == 0:
+            if step == 1:
                 sort_layer1(NET_F)
             if step == 2:
                 widen_b2(NET_O)
                 widen_b2(NET_F)
             if step + LOAD_AHEAD > 2 and job_at(step + LOAD_AHEAD)[0] == NET_O:
                 load_x(job_at(step + LOAD_AHEAD)[1])
+            if step == FIRST_BLEND:
+                drain()
             layer2(step - 2)
             layer1(step)
+            if step == 0:
+                relu(0)
+                transpose_x(1)
             copy_x(step + 1)
-            transpose_x(step + 2)
-            share_o(step - 4)
+            if step != -1:
+                transpose_x(step + 2)
+            for g in blends_at(step):
+                share_o(g)
+            four_times_max(step - 3)
             exponentials(step - 3)
-            relu(step)
-            invert_sum_f(step - 4)
+            if step != 0:
+                relu(step)
             tick()
             interleave(step - 1)
-            prepare_blend(step - 4)
             tick()
             add_b2(step - 2)
             tick()
@@ -530,12 +518,16 @@ def tile_combnethe_pa_t_kernel(
             tick()
             quantise_x(step + 1)
             tick()
+            for g in blends_at(step):
+                invert_sum_f(g)
             quantise_h(step - 1)
             tick()
+            for g in blends_at(step):
+                prepare_blend(g)
             find_max(step - 2)
             tick()
-            blend(step - 4)
+            for g in blends_at(step):
+                blend(g)
             tick()
-            four_times_max(step - 2)
-            tick()
-            gate_after(step - 4)
+            if step - 4 == N_GROUPS - 1:
+                gate()

@@ -43,9 +43,12 @@ def job_at(index):
 
 
 def vector_x_banks(g):
-    if g == 1:
-        return (0, 1)
-    return (1,) if g == 0 else ()
+    return (1,) if g <= 1 else ()
+
+
+def scalar_tiles(index):
+    net, g = job_at(index)
+    return 1 if net == NET_F and (g < N_GROUPS // 2 or g == N_GROUPS - 1) else 0
 
 
 def tile_combnethe_pa_t_kernel(
@@ -87,12 +90,13 @@ def tile_combnethe_pa_t_kernel(
         stats_4 = keep.tile([P, N_TILES // 2, 6], F32, name="stats_4")
         sum_f = keep.tile([P, N_TILES], F32, name="sum_f")
         gate_last = keep.tile([P, N_TILES], F32, name="gate_last")
+        inv_sum_f = keep.tile([P, N_TILES], F32, name="inv_sum_f")
+        coef_f = keep.tile([P, N_TILES], F32, name="coef_f")
         coef_o = keep.tile([P, N_TILES], F32, name="coef_o")
 
         w1_raw, w1_words, w1_scales, w2_words, w2_scales = {}, {}, {}, {}, {}
-        b1_raw, b1_col = {}, {}
+        b1_raw = {}
         b2_raw = keep.tile([P, 2, CLASSES], BF16, name="b2_raw")
-        b2_both = keep.tile([P, 2, CLASSES], F32, name="b2_both")
 
         def load_weight(words_in, scales_in, width, name):
             words = keep.tile([P, width], U32, name=name + "_words", align_bytes=64)
@@ -127,11 +131,6 @@ def tile_combnethe_pa_t_kernel(
                     out=sorted_tile[:].rearrange("k (t p) -> k t p", t=PACK),
                     in_=raw[:].rearrange("k (p t) -> k t p", t=PACK),
                 )
-            b1_col[net] = keep.tile([P, PACK], F32, name="b1_col_%d" % net)
-            nc.vector.tensor_copy(out=b1_col[net][:], in_=b1_raw[net][:])
-
-        def widen_b2(net):
-            nc.vector.tensor_copy(out=b2_both[:, net, :], in_=b2_raw[:, net, :])
 
         x_loaded, x_banks, x_grouped, z_banks, hidden, h_grouped, h_packed = {}, {}, {}, {}, {}, {}, {}
         logit_banks, logits, neg_max, exp_f = {}, {}, {}, {}
@@ -210,7 +209,7 @@ def tile_combnethe_pa_t_kernel(
                 return
             h = h_pool.tile([P, PACK, WIDE], BF16, name="h")
             for t in range(PACK):
-                z, b1 = z_banks[(net, g, t)], b1_col[net][:, t : t + 1]
+                z, b1 = z_banks[(net, g, t)], b1_raw[net][:, t : t + 1]
                 if index == 0 and t >= 2:
                     nc.vector.tensor_scalar(
                         out=h[:, t, :], in0=z[:], scalar1=b1, scalar2=0.0, op0=ALU.add, op1=ALU.max
@@ -219,17 +218,17 @@ def tile_combnethe_pa_t_kernel(
                     nc.scalar.activation(out=h[:, t, :], in_=z[:], func=ACT.Relu, bias=b1, scale=1.0)
             hidden[(net, g)] = h
 
-        def interleave(index):
+        def interleave(copy, index, first, last):
             net, g = job_at(index)
-            if net is None:
+            if net is None or first == last:
                 return
-            h = hidden[(net, g)]
-            grouped = h_grouped_pool.tile([P, WIDE, PACK], BF16, name="h_grouped", align_bytes=64)
-            nc.vector.tensor_copy(
-                out=grouped[:].rearrange("p (c i) t -> p c t i", i=4),
-                in_=h[:].rearrange("p t (c i) -> p c t i", i=4),
+            if (net, g) not in h_grouped:
+                h_grouped[(net, g)] = h_grouped_pool.tile([P, WIDE, PACK], BF16, name="h_grouped", align_bytes=64)
+            tokens = slice(first * P, last * P)
+            copy(
+                out=h_grouped[(net, g)][:, tokens, :].rearrange("p (c i) t -> p c t i", i=4),
+                in_=hidden[(net, g)][:, :, tokens].rearrange("p t (c i) -> p c t i", i=4),
             )
-            h_grouped[(net, g)] = grouped
 
         def quantise_h(index):
             net, g = job_at(index)
@@ -271,7 +270,7 @@ def tile_combnethe_pa_t_kernel(
             nc.vector.tensor_tensor(
                 out=zb[:],
                 in0=logit_banks[(net, g)][:],
-                in1=b2_both[:, net, :].unsqueeze(1).to_broadcast([P, GROUP, CLASSES]),
+                in1=b2_raw[:, net, :].unsqueeze(1).to_broadcast([P, GROUP, CLASSES]),
                 op=ALU.add,
             )
             logits[(net, g)] = zb
@@ -430,7 +429,7 @@ def tile_combnethe_pa_t_kernel(
             affine(rest[:], gate_last[:], -COND_SCALE / n, 1.0 / n)
             times(coef_o[:], rest[:], r1[:])
 
-        inv_sum_f, coef_f, shares = {}, {}, {}
+        shares = {}
 
         def blends_at(step):
             first = len(JOBS) - N_GROUPS
@@ -445,22 +444,23 @@ def tile_combnethe_pa_t_kernel(
                 )
             shares[g] = share
 
-        def invert_sum_f(g):
-            inverse = blend_pool.tile([P, GROUP], F32, name="inv_sum_f")
-            nc.vector.reciprocal(out=inverse[:], in_=sum_f[:, g * GROUP : (g + 1) * GROUP])
-            inv_sum_f[g] = inverse
+        def tiles_of(groups):
+            return slice(groups[0] * GROUP, (groups[-1] + 1) * GROUP)
 
-        def prepare_blend(g):
-            coef = blend_pool.tile([P, GROUP], F32, name="coef_f")
-            nc.vector.scalar_tensor_tensor(
-                out=coef[:],
-                in0=inv_sum_f[g][:],
-                scalar=COND_SCALE,
-                in1=gate_last[:, g * GROUP : (g + 1) * GROUP],
-                op0=ALU.mult,
-                op1=ALU.mult,
-            )
-            coef_f[g] = coef
+        def invert_sum_f(groups):
+            if groups:
+                nc.vector.reciprocal(out=inv_sum_f[:, tiles_of(groups)], in_=sum_f[:, tiles_of(groups)])
+
+        def prepare_blend(groups):
+            if groups:
+                nc.vector.scalar_tensor_tensor(
+                    out=coef_f[:, tiles_of(groups)],
+                    in0=inv_sum_f[:, tiles_of(groups)],
+                    scalar=COND_SCALE,
+                    in1=gate_last[:, tiles_of(groups)],
+                    op0=ALU.mult,
+                    op1=ALU.mult,
+                )
 
         def blend(g):
             result = blend_pool.tile([P, GROUP, CLASSES], F32, name="result")
@@ -468,7 +468,7 @@ def tile_combnethe_pa_t_kernel(
                 nc.vector.scalar_tensor_tensor(
                     out=result[:, j, :],
                     in0=exp_f[g][:, j, :],
-                    scalar=coef_f[g][:, j : j + 1],
+                    scalar=coef_f[:, g * GROUP + j : g * GROUP + j + 1],
                     in1=shares[g][:, j, :],
                     op0=ALU.mult,
                     op1=ALU.add,
@@ -484,13 +484,8 @@ def tile_combnethe_pa_t_kernel(
         load_layer2(NET_F)
 
         for step in range(-2, len(JOBS) + 4):
-            if step == -1:
-                sort_layer1(NET_O)
             if step == 1:
                 sort_layer1(NET_F)
-            if step == 2:
-                widen_b2(NET_O)
-                widen_b2(NET_F)
             if step + LOAD_AHEAD > 2 and job_at(step + LOAD_AHEAD)[0] == NET_O:
                 load_x(job_at(step + LOAD_AHEAD)[1])
             if step == FIRST_BLEND:
@@ -509,21 +504,22 @@ def tile_combnethe_pa_t_kernel(
             exponentials(step - 3)
             if step != 0:
                 relu(step)
+            interleave(nc.scalar.copy, step, 0, scalar_tiles(step))
             tick()
-            interleave(step - 1)
+            interleave(nc.vector.tensor_copy, step - 1, scalar_tiles(step - 1), GROUP)
             tick()
             add_b2(step - 2)
             tick()
             statistics(step - 4)
             tick()
             quantise_x(step + 1)
+            if step == -1:
+                sort_layer1(NET_O)
             tick()
-            for g in blends_at(step):
-                invert_sum_f(g)
+            invert_sum_f(blends_at(step))
             quantise_h(step - 1)
             tick()
-            for g in blends_at(step):
-                prepare_blend(g)
+            prepare_blend(blends_at(step))
             find_max(step - 2)
             tick()
             for g in blends_at(step):

@@ -43,12 +43,12 @@ def job_at(index):
 
 
 def vector_x_banks(g):
-    return (1,) if g <= 1 else ()
+    return (1,) if g == 1 else ()
 
 
 def scalar_tiles(index):
     net, g = job_at(index)
-    return 1 if net == NET_F and (g < N_GROUPS // 2 or g == N_GROUPS - 1) else 0
+    return (2 if g == N_GROUPS - 1 else 1) if net == NET_F and (g < N_GROUPS // 2 or g == N_GROUPS - 1) else 0
 
 
 def tile_combnethe_pa_t_kernel(
@@ -484,6 +484,8 @@ def tile_combnethe_pa_t_kernel(
         load_layer2(NET_F)
 
         for step in range(-2, len(JOBS) + 4):
+            if step == -1:
+                sort_layer1(NET_O)
             if step == 1:
                 sort_layer1(NET_F)
             if step + LOAD_AHEAD > 2 and job_at(step + LOAD_AHEAD)[0] == NET_O:
@@ -513,8 +515,6 @@ def tile_combnethe_pa_t_kernel(
             statistics(step - 4)
             tick()
             quantise_x(step + 1)
-            if step == -1:
-                sort_layer1(NET_O)
             tick()
             invert_sum_f(blends_at(step))
             quantise_h(step - 1)

@@ -226,8 +226,8 @@ def tile_combnethe_pa_t_kernel(
                 h_grouped[(net, g)] = h_grouped_pool.tile([P, WIDE, PACK], BF16, name="h_grouped", align_bytes=64)
             tokens = slice(first * P, last * P)
             copy(
-                out=h_grouped[(net, g)][:, tokens, :].rearrange("p (c i) t -> p c t i", i=4),
-                in_=hidden[(net, g)][:, :, tokens].rearrange("p t (c i) -> p c t i", i=4),
+                out=h_grouped[(net, g)][:, tokens, :].rearrange("p (c i) t -> p c t i", i=8),
+                in_=hidden[(net, g)][:, :, tokens].rearrange("p t (c i) -> p c t i", i=8),
             )
 
         def quantise_h(index):

from contextlib import ExitStack

import concourse.mybir as mybir
from concourse.masks import make_identity

F32 = mybir.dt.float32
BF16 = mybir.dt.bfloat16
I32 = mybir.dt.int32
U32 = mybir.dt.uint32
U8 = mybir.dt.uint8
FP8X4 = mybir.dt.float8_e4m3fn_x4
ALU = mybir.AluOpType
ACT = mybir.ActivationFunctionType
AXIS = mybir.AxisListType

P = 128
PACK = 4
TOKENS, D_IN, D_H, CLASSES = 8192, 512, 512, 128
N_TILES = TOKENS // P
GROUP = 4
WIDE = GROUP * P
N_GROUPS = N_TILES // GROUP
NET_O, NET_F = 0, 1
LOAD_AHEAD = 5
FIRST_BLEND = 25

TAU = 0.5
C0 = 2.0 / (2.0 + TAU * TAU)
COND_SCALE = C0**4 * TAU**8

FLOPS = 2 * 2 * TOKENS * (D_IN * D_H + D_H * CLASSES)


def all_jobs():
    return [(net, g) for net in (NET_O, NET_F) for g in range(N_GROUPS)]


JOBS = all_jobs()


def job_at(index):
    return JOBS[index] if 0 <= index < len(JOBS) else (None, None)


def vector_x_banks(g):
    return (1,) if g == 1 else ()


def scalar_tiles(index):
    net, g = job_at(index)
    return (2 if g == N_GROUPS - 1 else 1) if net == NET_F and (g < N_GROUPS // 2 or g == N_GROUPS - 1) else 0


def tile_combnethe_pa_t_kernel(
    tc, x, W1o_words, W1o_scales, b1o, W2o_words, W2o_scales, b2o,
    W1f_words, W1f_scales, b1f, W2f_words, W2f_scales, b2f, out,
):
    nc = tc.nc
    weights_in = {
        NET_O: (W1o_words, W1o_scales, b1o, W2o_words, W2o_scales, b2o),
        NET_F: (W1f_words, W1f_scales, b1f, W2f_words, W2f_scales, b2f),
    }
    x_by_tile = x.rearrange("(p i) k -> p i k", i=N_TILES)
    out_by_tile = out.rearrange("(p i) c -> p i c", i=N_TILES)

    with ExitStack() as ctx:
        ctx.enter_context(tc.manual_schedule())
        keep = ctx.enter_context(tc.tile_pool(name="keep", bufs=1))
        loads = ctx.enter_context(tc.tile_pool(name="loads", bufs=6))
        x_grouped_pool = ctx.enter_context(tc.tile_pool(name="x_grouped", bufs=3))
        h_pool = ctx.enter_context(tc.tile_pool(name="h", bufs=3))
        h_grouped_pool = ctx.enter_context(tc.tile_pool(name="h_grouped", bufs=3))
        h_packed_pool = ctx.enter_context(tc.tile_pool(name="h_packed", bufs=3))
        logit_pool = ctx.enter_context(tc.tile_pool(name="logit", bufs=3))
        exp_o4_pool = ctx.enter_context(tc.tile_pool(name="exp_o4", bufs=3))
        exp_f_pool = ctx.enter_context(tc.tile_pool(name="exp_f", bufs=9))
        blend_pool = ctx.enter_context(tc.tile_pool(name="blend", bufs=3))
        gate_pool = ctx.enter_context(tc.tile_pool(name="gate", bufs=1))
        psum_x = ctx.enter_context(tc.psum_pool(name="psum_x", bufs=2))
        psum_z = ctx.enter_context(tc.psum_pool(name="psum_z", bufs=4))
        psum_l = ctx.enter_context(tc.psum_pool(name="psum_l", bufs=2))

        identity = keep.tile([P, P], F32, name="identity")
        make_identity(nc, identity[:])

        x_words = keep.tile([P, TOKENS], U32, name="x_words", align_bytes=64)
        x_scales = keep.tile([P, TOKENS], U8, name="x_scales", align_bytes=64)
        exp_o = keep.tile([P, N_TILES, CLASSES], F32, name="exp_o")
        stats_1 = keep.tile([P, N_TILES // 2, 6], F32, name="stats_1")
        stats_4 = keep.tile([P, N_TILES // 2, 6], F32, name="stats_4")
        sum_f = keep.tile([P, N_TILES], F32, name="sum_f")
        gate_last = keep.tile([P, N_TILES], F32, name="gate_last")
        inv_sum_f = keep.tile([P, N_TILES], F32, name="inv_sum_f")
        coef_f = keep.tile([P, N_TILES], F32, name="coef_f")
        coef_o = keep.tile([P, N_TILES], F32, name="coef_o")

        w1_raw, w1_words, w1_scales, w2_words, w2_scales = {}, {}, {}, {}, {}
        b1_raw = {}
        b2_raw = keep.tile([P, 2, CLASSES], BF16, name="b2_raw")

        def load_weight(words_in, scales_in, width, name):
            words = keep.tile([P, width], U32, name=name + "_words", align_bytes=64)
            nc.sync.dma_start(
                out=words[:].bitcast(I32), in_=words_in[0].rearrange("p n t -> p (n t)").bitcast(I32)
            )
            scales = keep.tile([P, width], U8, name=name + "_scales", align_bytes=64)
            nc.vector.memset(scales[:].bitcast(I32), 0)
            for r in range(4):
                nc.sync.dma_start(
                    out=scales[:].bitcast(I32)[r:P:32, :], in_=scales_in[0].bitcast(I32)[r:16:4, :]
                )
            return words, scales

        def load_layer1(net):
            w1w, w1s, b1, w2w, w2s, b2 = weights_in[net]
            w1_raw[net] = load_weight(w1w, w1s, D_H, "w1_raw_%d" % net)
            b1_raw[net] = keep.tile([P, PACK], BF16, name="b1_raw_%d" % net)
            nc.sync.dma_start(out=b1_raw[net][:], in_=b1.rearrange("(p t) -> p t", t=PACK))

        def load_layer2(net):
            w1w, w1s, b1, w2w, w2s, b2 = weights_in[net]
            w2_words[net], w2_scales[net] = load_weight(w2w, w2s, CLASSES, "w2_%d" % net)
            nc.sync.dma_start(out=b2_raw[:, net, :], in_=b2.partition_broadcast(P))

        def sort_layer1(net):
            words, scales = w1_raw[net]
            w1_words[net] = keep.tile([P, D_H], U32, name="w1_words_%d" % net, align_bytes=64)
            w1_scales[net] = keep.tile([P, D_H], U8, name="w1_scales_%d" % net, align_bytes=64)
            for sorted_tile, raw in ((w1_words[net], words), (w1_scales[net], scales)):
                nc.vector.tensor_copy(
                    out=sorted_tile[:].rearrange("k (t p) -> k t p", t=PACK),
                    in_=raw[:].rearrange("k (p t) -> k t p", t=PACK),
                )

        x_loaded, x_banks, x_grouped, z_banks, hidden, h_grouped, h_packed = {}, {}, {}, {}, {}, {}, {}
        logit_banks, logits, neg_max, exp_f = {}, {}, {}, {}

        def load_x(g, pieces=1):
            if not 0 <= g < N_GROUPS:
                return
            x_rows = loads.tile([P, GROUP, D_IN], BF16, name="x_rows")
            n = GROUP // pieces
            for j in range(0, GROUP, n):
                nc.sync.dma_start(
                    out=x_rows[:, j : j + n, :], in_=x_by_tile[:, g * GROUP + j : g * GROUP + j + n, :]
                )
            x_loaded[g] = x_rows

        def transpose_x(index):
            net, g = job_at(index)
            if net != NET_O:
                return
            words = x_loaded[g][:].rearrange("p i k -> p (i k)").bitcast(F32)
            words_per_tile = D_IN // 2
            for half in range(2):
                xt = psum_x.tile([P, 2, 2, P], F32, name="xt")
                for j in range(2):
                    start = (half * 2 + j) * words_per_tile
                    for u in range(2):
                        nc.tensor.transpose(
                            out=xt[:, j, u, :],
                            in_=words[:, start + u : start + words_per_tile : 2],
                            identity=identity[:],
                        )
                x_banks[(g, half)] = xt

        def copy_x(index):
            net, g = job_at(index)
            if net != NET_O:
                return
            grouped = x_grouped_pool.tile([P, WIDE * PACK], BF16, name="x_grouped", align_bytes=64)
            side_by_side = grouped[:].bitcast(F32).rearrange("p (h j w u) -> p h j w u", h=2, j=2, u=2)
            for half in range(2):
                copy = nc.vector.tensor_copy if half in vector_x_banks(g) else nc.scalar.copy
                copy(out=side_by_side[:, half, :, :, :], in_=x_banks[(g, half)][:].rearrange("p j u w -> p j w u"))
            x_grouped[g] = grouped

        def quantise_x(index):
            net, g = job_at(index)
            if net != NET_O:
                return
            cols = slice(g * WIDE, (g + 1) * WIDE)
            nc.vector.quantize_mx(
                out=x_words[:, cols].bitcast(FP8X4), scales=x_scales[:, cols], in_=x_grouped[g][:]
            )

        def layer1(index):
            net, g = job_at(index)
            if net is None:
                return
            cols = slice(g * WIDE, (g + 1) * WIDE)
            for t in range(PACK):
                units = slice(t * P, (t + 1) * P)
                z = psum_z.tile([P, WIDE], F32, name="z")
                nc.tensor.matmul_mx(
                    out=z[:],
                    lhsT=w1_words[net][:, units].bitcast(FP8X4),
                    lhsT_scale=w1_scales[net][:, units],
                    rhs=x_words[:, cols].bitcast(FP8X4),
                    rhs_scale=x_scales[:, cols],
                    start=True,
                    stop=True,
                )
                z_banks[(net, g, t)] = z

        def relu(index):
            net, g = job_at(index)
            if net is None:
                return
            h = h_pool.tile([P, PACK, WIDE], BF16, name="h")
            for t in range(PACK):
                z, b1 = z_banks[(net, g, t)], b1_raw[net][:, t : t + 1]
                if index == 0 and t >= 2:
                    nc.vector.tensor_scalar(
                        out=h[:, t, :], in0=z[:], scalar1=b1, scalar2=0.0, op0=ALU.add, op1=ALU.max
                    )
                else:
                    nc.scalar.activation(out=h[:, t, :], in_=z[:], func=ACT.Relu, bias=b1, scale=1.0)
            hidden[(net, g)] = h

        def interleave(copy, index, first, last):
            net, g = job_at(index)
            if net is None or first == last:
                return
            if (net, g) not in h_grouped:
                h_grouped[(net, g)] = h_grouped_pool.tile([P, WIDE, PACK], BF16, name="h_grouped", align_bytes=64)
            tokens = slice(first * P, last * P)
            copy(
                out=h_grouped[(net, g)][:, tokens, :].rearrange("p (c i) t -> p c t i", i=8),
                in_=hidden[(net, g)][:, :, tokens].rearrange("p t (c i) -> p c t i", i=8),
            )

        def quantise_h(index):
            net, g = job_at(index)
            if net is None:
                return
            h_words = h_packed_pool.tile([P, WIDE], U32, name="h_words", align_bytes=64)
            h_scales = h_packed_pool.tile([P, WIDE], U8, name="h_scales", align_bytes=64)
            nc.vector.quantize_mx(
                out=h_words[:].bitcast(FP8X4),
                scales=h_scales[:],
                in_=h_grouped[(net, g)][:].rearrange("p n t -> p (n t)"),
            )
            h_packed[(net, g)] = (h_words, h_scales)

        def layer2(index):
            net, g = job_at(index)
            if net is None:
                return
            bank = psum_l.tile([P, GROUP, CLASSES], F32, name="logit_bank")
            h_words, h_scales = h_packed[(net, g)]
            for j in range(GROUP):
                cols = slice(j * P, (j + 1) * P)
                nc.tensor.matmul_mx(
                    out=bank[:, j, :],
                    lhsT=h_words[:, cols].bitcast(FP8X4),
                    lhsT_scale=h_scales[:, cols],
                    rhs=w2_words[net][:].bitcast(FP8X4),
                    rhs_scale=w2_scales[net][:],
                    start=True,
                    stop=True,
                )
            logit_banks[(net, g)] = bank

        def add_b2(index):
            net, g = job_at(index)
            if net is None:
                return
            zb = logit_pool.tile([P, GROUP, CLASSES], F32, name="zb")
            nc.vector.tensor_tensor(
                out=zb[:],
                in0=logit_banks[(net, g)][:],
                in1=b2_raw[:, net, :].unsqueeze(1).to_broadcast([P, GROUP, CLASSES]),
                op=ALU.add,
            )
            logits[(net, g)] = zb

        def find_max(index):
            net, g = job_at(index)
            if net is None:
                return
            minus_max = logit_pool.tile([P, GROUP], F32, name="minus_max")
            nc.vector.tensor_reduce(out=minus_max[:], in_=logits[(net, g)][:], axis=AXIS.X, op=ALU.max, negate=True)
            neg_max[(net, g)] = minus_max

        exp_o4, neg_max4 = {}, {}

        def four_times_max(index):
            net, g = job_at(index)
            if net != NET_O:
                return
            minus_max4 = logit_pool.tile([P, GROUP], F32, name="minus_max4")
            nc.scalar.activation(out=minus_max4[:], in_=neg_max[(net, g)][:], func=ACT.Copy, scale=4.0)
            neg_max4[g] = minus_max4

        def exponentials(index):
            net, g = job_at(index)
            if net == NET_F:
                exp_f[g] = exp_f_pool.tile([P, GROUP, CLASSES], F32, name="exp_f")
                for j in range(GROUP):
                    i = g * GROUP + j
                    nc.scalar.activation(
                        out=exp_f[g][:, j, :],
                        in_=logits[(net, g)][:, j, :],
                        func=ACT.Exp,
                        bias=neg_max[(net, g)][:, j : j + 1],
                        scale=1.0,
                        accum_out=sum_f[:, i : i + 1],
                    )
            if net == NET_O:
                exp_o4[g] = exp_o4_pool.tile([P, GROUP, CLASSES], F32, name="exp_o4")
                for j in range(GROUP):
                    nc.scalar.activation(
                        out=exp_o[:, g * GROUP + j, :],
                        in_=logits[(net, g)][:, j, :],
                        func=ACT.Exp,
                        bias=neg_max[(net, g)][:, j : j + 1],
                        scale=1.0,
                    )
                for j in range(GROUP):
                    nc.scalar.activation(
                        out=exp_o4[g][:, j, :],
                        in_=logits[(net, g)][:, j, :],
                        func=ACT.Exp,
                        bias=neg_max4[g][:, j : j + 1],
                        scale=4.0,
                    )

        def statistics(index):
            net, g = job_at(index)
            if net != NET_O:
                return
            for pair in range(GROUP // 2):
                j = 2 * pair
                i = g * GROUP + j
                nc.vector.bn_stats(
                    out=stats_1[:, i // 2, :], in_=exp_o[:, i : i + 2, :].rearrange("p j c -> p c j")
                )
                nc.vector.bn_stats(
                    out=stats_4[:, i // 2, :], in_=exp_o4[g][:, j : j + 2, :].rearrange("p j c -> p c j")
                )

        pending = []

        def tick():
            if pending:
                operation = pending[0]
                pending.remove(operation)
                operation()

        def drain():
            while pending:
                tick()

        def gate():
            n = float(CLASSES)

            def column(name):
                return gate_pool.tile([P, N_TILES], F32, name=name)

            def times(out, a, b):
                pending.append(lambda: nc.vector.tensor_tensor(out=out, in0=a, in1=b, op=ALU.mult))

            def affine(out, a, scale, shift):
                pending.append(
                    lambda: nc.vector.tensor_scalar(
                        out=out, in0=a, scalar1=scale, scalar2=shift, op0=ALU.mult, op1=ALU.add
                    )
                )

            def shifted_times(out, a, shift, b):
                pending.append(
                    lambda: nc.vector.scalar_tensor_tensor(
                        out=out, in0=a, scalar=shift, in1=b, op0=ALU.add, op1=ALU.mult
                    )
                )

            def series(tag, v, scale, shift):
                u = [column("u%d_%s" % (k, tag)) for k in range(4)]
                partial = [column("partial%d_%s" % (k, tag)) for k in range(3)]
                result = column("series_" + tag)
                affine(u[0][:], v, scale, shift)
                affine(partial[0][:], v, scale, shift + 1.0)
                for k in range(3):
                    times(u[k + 1][:], u[k][:], u[k][:])
                shifted_times(partial[1][:], u[1][:], 1.0, partial[0][:])
                shifted_times(partial[2][:], u[2][:], 1.0, partial[1][:])
                shifted_times(result[:], u[3][:], 1.0, partial[2][:])
                return result

            by_tile_1 = stats_1[:].rearrange("p q (j s) -> p (q j) s", s=3)
            by_tile_4 = stats_4[:].rearrange("p q (j s) -> p (q j) s", s=3)
            mean_1, deviation_1 = by_tile_1[:, :, 1], by_tile_1[:, :, 2]
            mean_4, deviation_4 = by_tile_4[:, :, 1], by_tile_4[:, :, 2]
            r1, r2, r4, r8 = column("r1"), column("r2"), column("r4"), column("r8")
            pending.append(lambda: nc.vector.reciprocal(out=r1[:], in_=mean_1))
            times(r2[:], r1[:], r1[:])
            times(r4[:], r2[:], r2[:])
            spread_1 = column("spread_1")
            times(spread_1[:], deviation_1, r2[:])
            times(r8[:], r4[:], r4[:])
            moment_4 = column("moment_4")
            times(moment_4[:], mean_4, r4[:])
            spread_4 = column("spread_4")
            times(spread_4[:], deviation_4, r8[:])
            moment_4_squared = column("moment_4_squared")
            times(moment_4_squared[:], moment_4[:], moment_4[:])
            moment_8 = column("moment_8")
            pending.append(
                lambda: nc.vector.scalar_tensor_tensor(
                    out=moment_8[:], in0=moment_4_squared[:], scalar=n, in1=spread_4[:], op0=ALU.mult, op1=ALU.add
                )
            )
            g0 = series("g0", spread_1[:], -C0 / n**2, 1.0 - C0 * (TAU**2 + 1.0 / n))
            g0_squared = column("g0_squared")
            times(g0_squared[:], g0[:], g0[:])
            sm1 = column("sm1")
            shifted_times(sm1[:], moment_4[:], TAU**4 * n**3, g0_squared[:])
            g1 = series("g1", sm1[:], -(C0**2) / n**3, 1.0)
            factor = column("factor")
            times(factor[:], g0_squared[:], g1[:])
            factor_squared = column("factor_squared")
            times(factor_squared[:], factor[:], factor[:])
            sm2 = column("sm2")
            shifted_times(sm2[:], moment_8[:], TAU**8 * n**8, factor_squared[:])
            g2 = series("g2", sm2[:], -(C0**4) / n**8, 1.0)
            times(gate_last[:], factor_squared[:], g2[:])
            rest = column("rest")
            affine(rest[:], gate_last[:], -COND_SCALE / n, 1.0 / n)
            times(coef_o[:], rest[:], r1[:])

        shares = {}

        def blends_at(step):
            first = len(JOBS) - N_GROUPS
            return [g for g in range(N_GROUPS) if max(first + g + 4, FIRST_BLEND + g // 2) == step]

        def share_o(g):
            share = blend_pool.tile([P, GROUP, CLASSES], F32, name="share")
            for j in range(GROUP):
                i = g * GROUP + j
                nc.scalar.activation(
                    out=share[:, j, :], in_=exp_o[:, i, :], func=ACT.Copy, scale=coef_o[:, i : i + 1]
                )
            shares[g] = share

        def tiles_of(groups):
            return slice(groups[0] * GROUP, (groups[-1] + 1) * GROUP)

        def invert_sum_f(groups):
            if groups:
                nc.vector.reciprocal(out=inv_sum_f[:, tiles_of(groups)], in_=sum_f[:, tiles_of(groups)])

        def prepare_blend(groups):
            if groups:
                nc.vector.scalar_tensor_tensor(
                    out=coef_f[:, tiles_of(groups)],
                    in0=inv_sum_f[:, tiles_of(groups)],
                    scalar=COND_SCALE,
                    in1=gate_last[:, tiles_of(groups)],
                    op0=ALU.mult,
                    op1=ALU.mult,
                )

        def blend(g):
            result = blend_pool.tile([P, GROUP, CLASSES], F32, name="result")
            for j in range(GROUP):
                nc.vector.scalar_tensor_tensor(
                    out=result[:, j, :],
                    in0=exp_f[g][:, j, :],
                    scalar=coef_f[:, g * GROUP + j : g * GROUP + j + 1],
                    in1=shares[g][:, j, :],
                    op0=ALU.mult,
                    op1=ALU.add,
                )
            nc.sync.dma_start(out=out_by_tile[:, g * GROUP : (g + 1) * GROUP, :], in_=result[:])

        load_x(0, pieces=2)
        load_layer1(NET_O)
        load_x(1)
        load_layer2(NET_O)
        load_x(2)
        load_layer1(NET_F)
        load_layer2(NET_F)

        for step in range(-2, len(JOBS) + 4):
            if step == -1:
                sort_layer1(NET_O)
            if step == 1:
                sort_layer1(NET_F)
            if step + LOAD_AHEAD > 2 and job_at(step + LOAD_AHEAD)[0] == NET_O:
                load_x(job_at(step + LOAD_AHEAD)[1])
            if step == FIRST_BLEND:
                drain()
            layer2(step - 2)
            layer1(step)
            if step == 0:
                relu(0)
                transpose_x(1)
            copy_x(step + 1)
            if step != -1:
                transpose_x(step + 2)
            for g in blends_at(step):
                share_o(g)
            four_times_max(step - 3)
            exponentials(step - 3)
            if step != 0:
                relu(step)
            interleave(nc.scalar.copy, step, 0, scalar_tiles(step))
            tick()
            interleave(nc.vector.tensor_copy, step - 1, scalar_tiles(step - 1), GROUP)
            tick()
            add_b2(step - 2)
            tick()
            statistics(step - 4)
            tick()
            quantise_x(step + 1)
            tick()
            invert_sum_f(blends_at(step))
            quantise_h(step - 1)
            tick()
            prepare_blend(blends_at(step))
            find_max(step - 2)
            tick()
            for g in blends_at(step):
                blend(g)
            tick()
            if step - 4 == N_GROUPS - 1:
                gate()
